import numpy as np
import ml_dtypes


def mxq(x, axis, fmt="e4m3"):
    dtype, down = {"e4m3": (ml_dtypes.float8_e4m3fn, 7), "e5m2": (ml_dtypes.float8_e5m2, 14)}[fmt]
    v = np.moveaxis(np.asarray(x, np.float32).astype(ml_dtypes.bfloat16).astype(np.float64), axis, -1)
    blocks = v.reshape(v.shape[:-1] + (-1, 32))
    amax = np.abs(blocks).max(-1, keepdims=True)
    byte = np.maximum(np.where(amax > 0, np.frexp(amax)[1] - 1 + 127, 0) - down, 1)
    scale = np.exp2(byte - 127.0)
    codes = (blocks / scale).astype(np.float32).astype(dtype).astype(np.float64)
    return np.moveaxis((codes * scale).reshape(v.shape), -1, axis)


WIDE = False


def mx_kscale(k):
    if not WIDE:
        return np.ones(k)
    levels = np.array([10, -10, 5, -5, 0])
    a = np.random.permutation(np.resize(levels, k // 512 * 4)).reshape(k // 512, 4)
    idx = np.arange(k)
    return np.exp2(a[idx // 512, idx % 128 // 32])


BF16 = ml_dtypes.bfloat16


def bf(x):
    return np.asarray(x, np.float32).astype(BF16)


def f64(x):
    return np.asarray(x).astype(np.float64)


E2M1 = np.array([0.0, 0.5, 1.0, 1.5, 2.0, 3.0, 4.0, 6.0, -0.0, -0.5, -1.0, -1.5, -2.0, -3.0, -4.0, -6.0])


def pack_weight(w, fmt):
    k, n = w.shape
    w = f64(bf(w)).reshape(k // 32, 32, n)
    amax = np.abs(w).max(1)
    if fmt == "e4m3":
        byte = np.frexp(amax)[1] - 1 + 127 - 7
    else:
        mant, ex = np.frexp(amax / 6.0)
        byte = np.where(mant > 0.5, ex, ex - 1) + 127
    byte = np.clip(np.where(amax > 0, byte, 1), 1, 254)
    scaled = (w * np.exp2(127.0 - byte)[:, None, :]).reshape(k, n).astype(np.float32)
    by_word = np.ascontiguousarray(scaled.reshape(k // 512, 128, 4, n).transpose(0, 1, 3, 2))
    if fmt == "e4m3":
        words = by_word.astype(ml_dtypes.float8_e4m3fn).view(np.uint8)
    else:
        c = by_word.astype(ml_dtypes.float4_e2m1fn).view(np.uint8) & 0xF
        words = c[..., 0::2] | (c[..., 1::2] << 4)
    return np.ascontiguousarray(words), np.ascontiguousarray(byte.astype(np.uint8).reshape(k // 512, 16, n))


def unpack_weight(words, scales, fmt):
    g, p, n, _ = words.shape
    if fmt == "e4m3":
        vals = np.ascontiguousarray(words).view(ml_dtypes.float8_e4m3fn).astype(np.float64)
    else:
        nib = np.empty((g, p, n, 4), np.uint8)
        nib[..., 0::2] = words & 0xF
        nib[..., 1::2] = words >> 4
        vals = E2M1[nib]
    vals = vals * np.repeat(np.exp2(scales.astype(np.float64) - 127.0), 8, axis=1)[..., None]
    return vals.transpose(0, 1, 3, 2).reshape(g * 512, n)

def pack4(w):
    words, scales = pack_weight(w, "e2m1")
    return words.reshape(words.shape[0], 128, -1), scales


def unpack4(words, scales):
    return unpack_weight(words.reshape(words.shape[0], 128, -1, 2), scales, "e2m1")


B, D, F, NB, R = 8192, 128, 512, 4, 512
C = NB * D


def silu(v):
    return v / (1.0 + np.exp(-v))


def setup_inputs():
    s, u = mx_kscale(C), mx_kscale(F)
    g0 = bf(np.random.standard_normal((B, F)) * 0.6 * u)
    w2_0_words, w2_0_scales = pack4((np.random.standard_normal((D, F)) * 0.5 / np.sqrt(F) / u).T)
    wk_rest = bf(np.random.standard_normal((B, NB, D)) * 0.3 * s.reshape(NB, D))
    fc1_w_words, fc1_w_scales = pack4((np.random.standard_normal((R, C)) * 3.0 / np.sqrt(C) / s).T)
    fc1_b = bf(np.random.standard_normal(R) * 0.5)
    fc2_w_words, fc2_w_scales = pack4((np.random.standard_normal((D, R)) * 0.5 / np.sqrt(R)).T)
    fc2_b = bf(np.random.standard_normal(D) * 0.15)
    return {"g0": g0,
            "w2_0_words": w2_0_words,
            "w2_0_scales": w2_0_scales,
            "wk_rest": wk_rest,
            "fc1_w_words": fc1_w_words,
            "fc1_w_scales": fc1_w_scales,
            "fc1_b": fc1_b,
            "fc2_w_words": fc2_w_words,
            "fc2_w_scales": fc2_w_scales,
            "fc2_b": fc2_b}


def reference(g0, w2_0_words, w2_0_scales, wk_rest, fc1_w_words, fc1_w_scales, fc1_b, fc2_w_words, fc2_w_scales, fc2_b):
    o0 = mxq(f64(g0), 1, "e4m3") @ unpack4(w2_0_words, w2_0_scales)
    concat = f64(wk_rest).reshape(B, C)
    h = silu((mxq(concat, 1, "e4m3") @ unpack4(fc1_w_words, fc1_w_scales)) + f64(fc1_b))
    proj = (mxq(h, 1, "e4m3") @ unpack4(fc2_w_words, fc2_w_scales)) + f64(fc2_b)
    diff = o0 - proj
    return np.sqrt((diff ** 2).sum(axis=1)), np.abs(diff).mean(axis=1)

@@ -1,0 +1,275 @@
+from contextlib import ExitStack
+
+import concourse.mybir as mybir
+from concourse.masks import make_identity
+
+BF16 = mybir.dt.bfloat16
+F32 = mybir.dt.float32
+I32 = mybir.dt.int32
+U32 = mybir.dt.uint32
+U8 = mybir.dt.uint8
+FP8X4 = mybir.dt.float8_e4m3fn_x4
+FP4X4 = mybir.dt.float4_e2m1fn_x4
+ACT = mybir.ActivationFunctionType
+ALU = mybir.AluOpType
+
+P = 128
+PACK = 4
+K = P * PACK
+ROWS = 8192
+HIDDEN = 512
+OUT = 128
+ROW_TILES = ROWS // P
+CHUNK_TILES = 4
+CHUNK = CHUNK_TILES * P
+CHUNKS = ROW_TILES // CHUNK_TILES
+HIDDEN_TILES = HIDDEN // P
+WORDS = K // 2
+BANK_TILES = 2
+BANKS = CHUNK_TILES // BANK_TILES
+
+FLOPS = 2 * ROWS * K * (OUT + HIDDEN + OUT)
+
+FC1_TURN = 1
+H_TURN = 3
+FC2_TURN = 4
+DIFF_TURN = 5
+LOAD_AHEAD = 3
+
+
+def tile_nnapprox_pa_t_kernel(
+    tc,
+    g0,
+    w2_0_words,
+    w2_0_scales,
+    wk_rest,
+    fc1_w_words,
+    fc1_w_scales,
+    fc1_b,
+    fc2_w_words,
+    fc2_w_scales,
+    fc2_b,
+    out_0,
+    out_1,
+):
+    nc = tc.nc
+    g0_rows = g0.rearrange("(p r) k -> p r k", r=ROW_TILES)
+    concat_rows = wk_rest.rearrange("(p r) n d -> p r (n d)", r=ROW_TILES)
+
+    with ExitStack() as ctx:
+        ctx.enter_context(tc.manual_schedule())
+        const = ctx.enter_context(tc.tile_pool(name="const", bufs=1))
+        loads = ctx.enter_context(tc.tile_pool(name="loads", bufs=LOAD_AHEAD + 1))
+        work = ctx.enter_context(tc.tile_pool(name="work", bufs=2))
+        moved = ctx.enter_context(tc.tile_pool(name="moved", bufs=H_TURN - FC1_TURN + 1))
+        t_psum = ctx.enter_context(tc.psum_pool(name="t_psum", bufs=3))
+        h_psum = ctx.enter_context(tc.psum_pool(name="h_psum", bufs=HIDDEN_TILES))
+        d_psum = ctx.enter_context(tc.psum_pool(name="d_psum", bufs=1))
+
+        tiles = {}
+
+        def live(chunk):
+            return 0 <= chunk < CHUNKS
+
+        def load(name, rows, chunk):
+            x = loads.tile([P, CHUNK_TILES, K], BF16, name=name, tag=name)
+            first = chunk * CHUNK_TILES
+            nc.sync.dma_start(out=x[:], in_=rows[:, first : first + CHUNK_TILES, :])
+            tiles[name, chunk] = x
+
+        def transpose(name, chunk):
+            x = tiles[name, chunk]
+            grouped = work.tile([P, CHUNK_TILES, P, PACK], BF16, name=name + "_grouped", tag=name + "_grouped", align_bytes=64)
+            tiles[name + "_grouped", chunk] = grouped
+            for half in range(BANKS):
+                bank = t_psum.tile([P, BANK_TILES, 2, P], F32, name="t_bank", tag="t_bank")
+                for r in range(BANK_TILES):
+                    words = x[:, half * BANK_TILES + r, :].bitcast(F32)
+                    for u in range(2):
+                        nc.tensor.transpose(bank[:, r, u, :], words[:, u:WORDS:2], ident[:])
+                tiles[name + "_bank", chunk, half] = bank
+
+        def empty_bank(copy, name, chunk, half):
+            bank = tiles[name + "_bank", chunk, half]
+            grouped = tiles[name + "_grouped", chunk]
+            first = half * BANK_TILES
+            copy(
+                out=grouped[:, first : first + BANK_TILES, :, :].bitcast(F32),
+                in_=bank[:].rearrange("p r u b -> p r b u"),
+            )
+
+        def quantise(name, chunk):
+            grouped = tiles[name + "_grouped", chunk]
+            codes = work.tile([P, CHUNK], U32, name=name + "_codes", tag=name + "_codes", align_bytes=64)
+            scales = work.tile([P, CHUNK], U8, name=name + "_scales", tag=name + "_scales", align_bytes=64)
+            nc.vector.quantize_mx(
+                out=codes[:].bitcast(FP8X4),
+                scales=scales[:],
+                in_=grouped[:].rearrange("p r b t -> p (r b t)"),
+            )
+            tiles[name + "_codes", chunk] = codes
+            tiles[name + "_scales", chunk] = scales
+
+        def fc1(chunk):
+            for j in range(HIDDEN_TILES):
+                bank = h_psum.tile([P, CHUNK], F32, name="h_bank", tag="h_bank")
+                nc.tensor.matmul_mx(
+                    out=bank[:],
+                    lhsT=fc1_words[:, 2 * P * j : 2 * P * (j + 1)].bitcast(FP4X4),
+                    lhsT_scale=weight_scales[:, P * j : P * (j + 1)],
+                    rhs=tiles["concat_codes", chunk][:].bitcast(FP8X4),
+                    rhs_scale=tiles["concat_scales", chunk][:],
+                    start=True,
+                    stop=True,
+                )
+                tiles["h_bank", chunk, j] = bank
+
+        def silu_and_move(chunk, j):
+            if j == 0:
+                tiles["h_t", chunk] = work.tile([P, HIDDEN_TILES, CHUNK], BF16, name="h_t", tag="h_t")
+                tiles["h_planes", chunk] = moved.tile([P, PACK, CHUNK], BF16, name="h_planes", tag="h_planes")
+            h_t = tiles["h_t", chunk]
+            nc.scalar.activation(
+                out=h_t[:, j, :], in_=tiles["h_bank", chunk, j][:], func=ACT.Silu, bias=fc1_bias[:, j : j + 1], scale=1.0
+            )
+            quarter = P // PACK
+            nc.sync.dma_start(out=tiles["h_planes", chunk][quarter * j : quarter * (j + 1), :, :], in_=h_t[:, j, :])
+
+        def regroup_h(chunk):
+            grouped = work.tile([P, CHUNK_TILES, P, PACK], BF16, name="h_grouped", tag="h_grouped", align_bytes=64)
+            nc.vector.tensor_scalar(
+                out=grouped[:].rearrange("p r (c i) t -> p (r c) t i", i=4),
+                in0=tiles["h_planes", chunk][:].rearrange("p t (c i) -> p c t i", i=4),
+                scalar1=-1.0,
+                scalar2=None,
+                op0=ALU.mult,
+            )
+            tiles["h_grouped", chunk] = grouped
+
+        def fc2_minus(chunk):
+            bank = d_psum.tile([P, CHUNK_TILES, OUT], F32, name="d_bank", tag="d_bank")
+            for r in range(CHUNK_TILES):
+                cols = slice(r * P, (r + 1) * P)
+                nc.tensor.matmul_mx(
+                    out=bank[:, r, :],
+                    lhsT=tiles["g0_codes", chunk][:, cols].bitcast(FP8X4),
+                    lhsT_scale=tiles["g0_scales", chunk][:, cols],
+                    rhs=w2_words[:].bitcast(FP4X4),
+                    rhs_scale=weight_scales[:, HIDDEN : HIDDEN + OUT],
+                    start=True,
+                    stop=False,
+                )
+                nc.tensor.matmul_mx(
+                    out=bank[:, r, :],
+                    lhsT=tiles["h_codes", chunk][:, cols].bitcast(FP8X4),
+                    lhsT_scale=tiles["h_scales", chunk][:, cols],
+                    rhs=fc2_words[:].bitcast(FP4X4),
+                    rhs_scale=weight_scales[:, HIDDEN + OUT : HIDDEN + 2 * OUT],
+                    start=False,
+                    stop=True,
+                )
+            tiles["d_bank", chunk] = bank
+
+        def subtract_bias(chunk):
+            diff = work.tile([P, CHUNK_TILES, OUT], F32, name="diff", tag="diff")
+            nc.vector.tensor_tensor(
+                out=diff[:],
+                in0=tiles["d_bank", chunk][:],
+                in1=fc2_bias[:].unsqueeze(1).to_broadcast([P, CHUNK_TILES, OUT]),
+                op=ALU.subtract,
+            )
+            tiles["diff", chunk] = diff
+
+        def sum_norms(chunk):
+            diff = tiles["diff", chunk]
+            for r in range(CHUNK_TILES):
+                col = chunk * CHUNK_TILES + r
+                nc.scalar.activation(out=unused[:], in_=diff[:, r, :], func=ACT.Square, accum_out=sum_sq[:, col : col + 1])
+                nc.scalar.activation(out=unused[:], in_=diff[:, r, :], func=ACT.Abs, accum_out=sum_abs[:, col : col + 1])
+
+        def load_weight(words, scales, words_tile, first_col):
+            cols = scales.shape[2]
+            nc.sync.dma_start(out=words_tile[:].bitcast(I32), in_=words[0].bitcast(I32))
+            for quad in range(4):
+                nc.sync.dma_start(
+                    out=weight_scales[32 * quad : 32 * quad + 4, first_col : first_col + cols].bitcast(I32),
+                    in_=scales[0, 4 * quad : 4 * quad + 4, :].bitcast(I32),
+                )
+
+        ident = const.tile([P, P], F32)
+        make_identity(nc, ident[:])
+
+        weight_scales = const.tile([P, HIDDEN + 2 * OUT], U8, align_bytes=64)
+        nc.vector.memset(weight_scales[:].bitcast(I32), 0)
+        fc1_words = const.tile([P, 2 * HIDDEN], U8, align_bytes=64)
+        w2_words = const.tile([P, 2 * OUT], U8, align_bytes=64)
+        fc2_words = const.tile([P, 2 * OUT], U8, align_bytes=64)
+
+        bias_rows = const.tile([P, P], BF16)
+        nc.vector.memset(bias_rows[:], 0.0)
+        nc.sync.dma_start(out=bias_rows[0:HIDDEN_TILES, :], in_=fc1_b.rearrange("(j m) -> j m", m=P))
+        for chunk in range(LOAD_AHEAD):
+            load("concat", concat_rows, chunk)
+            if chunk == 0:
+                load_weight(fc1_w_words, fc1_w_scales, fc1_words, 0)
+        load_weight(w2_0_words, w2_0_scales, w2_words, HIDDEN)
+        load_weight(fc2_w_words, fc2_w_scales, fc2_words, HIDDEN + OUT)
+        fc2_bias = const.tile([P, OUT], BF16)
+        nc.sync.dma_start(out=fc2_bias[:], in_=fc2_b.partition_broadcast(P))
+
+        bias_rows_f32 = const.tile([P, P], F32)
+        nc.vector.tensor_copy(out=bias_rows_f32[:], in_=bias_rows[:])
+        bias_bank = t_psum.tile([P, BANK_TILES, 2, P], F32, name="t_bank", tag="t_bank")
+        nc.tensor.transpose(bias_bank[:, 0, 0, :], bias_rows_f32[:], ident[:])
+        fc1_bias = const.tile([P, HIDDEN_TILES], F32)
+        nc.vector.tensor_copy(out=fc1_bias[:], in_=bias_bank[:, 0, 0, 0:HIDDEN_TILES])
+
+        sum_sq = const.tile([P, ROW_TILES], F32)
+        sum_abs = const.tile([P, ROW_TILES], F32)
+        unused = const.tile([P, OUT], F32)
+
+        for turn in range(CHUNKS + DIFF_TURN):
+            if live(turn + LOAD_AHEAD):
+                load("concat", concat_rows, turn + LOAD_AHEAD)
+            if live(turn - H_TURN + LOAD_AHEAD):
+                load("g0", g0_rows, turn - H_TURN + LOAD_AHEAD)
+
+            if live(turn - FC2_TURN):
+                quantise("g0", turn - FC2_TURN)
+            if live(turn - DIFF_TURN):
+                subtract_bias(turn - DIFF_TURN)
+
+            if live(turn):
+                transpose("concat", turn)
+                empty_bank(nc.vector.tensor_copy, "concat", turn, 0)
+            if live(turn - H_TURN):
+                regroup_h(turn - H_TURN)
+            if live(turn):
+                empty_bank(nc.vector.tensor_copy, "concat", turn, 1)
+            if live(turn - H_TURN):
+                quantise("h", turn - H_TURN)
+            if live(turn):
+                quantise("concat", turn)
+
+            if live(turn - FC1_TURN):
+                fc1(turn - FC1_TURN)
+            if live(turn - H_TURN):
+                transpose("g0", turn - H_TURN)
+            for half in range(BANKS):
+                if live(turn - FC1_TURN):
+                    silu_and_move(turn - FC1_TURN, 2 * half)
+                    silu_and_move(turn - FC1_TURN, 2 * half + 1)
+                if live(turn - H_TURN):
+                    empty_bank(nc.scalar.copy, "g0", turn - H_TURN, half)
+
+            if live(turn - FC2_TURN):
+                fc2_minus(turn - FC2_TURN)
+            if live(turn - DIFF_TURN):
+                sum_norms(turn - DIFF_TURN)
+
+        l2 = const.tile([P, ROW_TILES], F32)
+        nc.scalar.activation(out=l2[:], in_=sum_sq[:], func=ACT.Sqrt)
+        l1 = const.tile([P, ROW_TILES], F32)
+        nc.vector.tensor_scalar(out=l1[:], in0=sum_abs[:], scalar1=1.0 / OUT, scalar2=None, op0=ALU.mult)
+        nc.sync.dma_start(out=out_0.rearrange("(p r) -> p r", r=ROW_TILES), in_=l2[:])
+        nc.sync.dma_start(out=out_1.rearrange("(p r) -> p r", r=ROW_TILES), in_=l1[:])

@@ -116,7 +116,7 @@ def tile_nnapprox_pa_t_kernel(
                 nc.tensor.matmul_mx(
                     out=bank[:],
                     lhsT=fc1_words[:, 2 * P * j : 2 * P * (j + 1)].bitcast(FP4X4),
-                    lhsT_scale=weight_scales[:, P * j : P * (j + 1)],
+                    lhsT_scale=fc1_scales[:, P * j : P * (j + 1)],
                     rhs=tiles["concat_codes", chunk][:].bitcast(FP8X4),
                     rhs_scale=tiles["concat_scales", chunk][:],
                     start=True,
@@ -132,8 +132,7 @@ def tile_nnapprox_pa_t_kernel(
             nc.scalar.activation(
                 out=h_t[:, j, :], in_=tiles["h_bank", chunk, j][:], func=ACT.Silu, bias=fc1_bias[:, j : j + 1], scale=1.0
             )
-            quarter = P // PACK
-            nc.sync.dma_start(out=tiles["h_planes", chunk][quarter * j : quarter * (j + 1), :, :], in_=h_t[:, j, :])
+            nc.sync.dma_start(out=tiles["h_planes", chunk][j:P:HIDDEN_TILES, :, :], in_=h_t[:, j, :])
 
         def regroup_h(chunk):
             grouped = work.tile([P, CHUNK_TILES, P, PACK], BF16, name="h_grouped", tag="h_grouped", align_bytes=64)
@@ -201,17 +200,19 @@ def tile_nnapprox_pa_t_kernel(
 
         weight_scales = const.tile([P, HIDDEN + 2 * OUT], U8, align_bytes=64)
         nc.vector.memset(weight_scales[:].bitcast(I32), 0)
-        fc1_words = const.tile([P, 2 * HIDDEN], U8, align_bytes=64)
+        fc1_words_in = const.tile([P, 2 * HIDDEN], U8, align_bytes=64)
         w2_words = const.tile([P, 2 * OUT], U8, align_bytes=64)
         fc2_words = const.tile([P, 2 * OUT], U8, align_bytes=64)
 
         bias_rows = const.tile([P, P], BF16)
         nc.vector.memset(bias_rows[:], 0.0)
-        nc.sync.dma_start(out=bias_rows[0:HIDDEN_TILES, :], in_=fc1_b.rearrange("(j m) -> j m", m=P))
+        nc.sync.dma_start(
+            out=bias_rows[0:HIDDEN_TILES, :].rearrange("j (a t) -> j a t", t=PACK),
+            in_=fc1_b.rearrange("(a j t) -> j a t", j=HIDDEN_TILES, t=PACK),
+        )
+        load_weight(fc1_w_words, fc1_w_scales, fc1_words_in, 0)
         for chunk in range(LOAD_AHEAD):
             load("concat", concat_rows, chunk)
-            if chunk == 0:
-                load_weight(fc1_w_words, fc1_w_scales, fc1_words, 0)
         load_weight(w2_0_words, w2_0_scales, w2_words, HIDDEN)
         load_weight(fc2_w_words, fc2_w_scales, fc2_words, HIDDEN + OUT)
         fc2_bias = const.tile([P, OUT], BF16)
@@ -223,6 +224,17 @@ def tile_nnapprox_pa_t_kernel(
         nc.tensor.transpose(bias_bank[:, 0, 0, :], bias_rows_f32[:], ident[:])
         fc1_bias = const.tile([P, HIDDEN_TILES], F32)
         nc.vector.tensor_copy(out=fc1_bias[:], in_=bias_bank[:, 0, 0, 0:HIDDEN_TILES])
+
+        fc1_words = const.tile([P, 2 * HIDDEN], U8, align_bytes=64)
+        nc.vector.tensor_copy(
+            out=fc1_words[:].bitcast(I32).rearrange("p (j a w) -> p j a w", j=HIDDEN_TILES, w=2),
+            in_=fc1_words_in[:].bitcast(I32).rearrange("p (a j w) -> p j a w", j=HIDDEN_TILES, w=2),
+        )
+        fc1_scales = const.tile([P, HIDDEN], U8, align_bytes=64)
+        nc.vector.tensor_copy(
+            out=fc1_scales[:].bitcast(I32).rearrange("p (j a) -> p j a", j=HIDDEN_TILES),
+            in_=weight_scales[:, 0:HIDDEN].bitcast(I32).rearrange("p (a j) -> p j a", j=HIDDEN_TILES),
+        )
 
         sum_sq = const.tile([P, ROW_TILES], F32)
         sum_abs = const.tile([P, ROW_TILES], F32)

@@ -34,7 +34,8 @@ FC1_TURN = 1
 H_TURN = 3
 FC2_TURN = 4
 DIFF_TURN = 5
-LOAD_AHEAD = 3
+LOAD_CHUNKS = 2
+LOADS = CHUNKS // LOAD_CHUNKS
 
 
 def tile_nnapprox_pa_t_kernel(
@@ -59,7 +60,7 @@ def tile_nnapprox_pa_t_kernel(
     with ExitStack() as ctx:
         ctx.enter_context(tc.manual_schedule())
         const = ctx.enter_context(tc.tile_pool(name="const", bufs=1))
-        loads = ctx.enter_context(tc.tile_pool(name="loads", bufs=LOAD_AHEAD + 1))
+        loads = ctx.enter_context(tc.tile_pool(name="loads", bufs=LOADS))
         work = ctx.enter_context(tc.tile_pool(name="work", bufs=2))
         moved = ctx.enter_context(tc.tile_pool(name="moved", bufs=H_TURN - FC1_TURN + 1))
         t_psum = ctx.enter_context(tc.psum_pool(name="t_psum", bufs=3))
@@ -71,11 +72,14 @@ def tile_nnapprox_pa_t_kernel(
         def live(chunk):
             return 0 <= chunk < CHUNKS
 
-        def load(name, rows, chunk):
-            x = loads.tile([P, CHUNK_TILES, K], BF16, name=name, tag=name)
-            first = chunk * CHUNK_TILES
-            nc.sync.dma_start(out=x[:], in_=rows[:, first : first + CHUNK_TILES, :])
-            tiles[name, chunk] = x
+        def load(queue, name, rows, part):
+            x = loads.tile([P, LOAD_CHUNKS, CHUNK_TILES, K], BF16, name=name, tag=name)
+            first = part * LOAD_CHUNKS * CHUNK_TILES
+            queue.dma_start(
+                out=x[:].rearrange("p c r k -> p (c r) k"), in_=rows[:, first : first + LOAD_CHUNKS * CHUNK_TILES, :]
+            )
+            for c in range(LOAD_CHUNKS):
+                tiles[name, part * LOAD_CHUNKS + c] = x[:, c, :, :]
 
         def transpose(name, chunk):
             x = tiles[name, chunk]
@@ -195,6 +199,8 @@ def tile_nnapprox_pa_t_kernel(
                     in_=scales[0, 4 * quad : 4 * quad + 4, :].bitcast(I32),
                 )
 
+        load(nc.sync, "concat", concat_rows, 0)
+
         ident = const.tile([P, P], F32)
         make_identity(nc, ident[:])
 
@@ -211,12 +217,15 @@ def tile_nnapprox_pa_t_kernel(
             in_=fc1_b.rearrange("(a j t) -> j a t", j=HIDDEN_TILES, t=PACK),
         )
         load_weight(fc1_w_words, fc1_w_scales, fc1_words_in, 0)
-        for chunk in range(LOAD_AHEAD):
-            load("concat", concat_rows, chunk)
         load_weight(w2_0_words, w2_0_scales, w2_words, HIDDEN)
         load_weight(fc2_w_words, fc2_w_scales, fc2_words, HIDDEN + OUT)
         fc2_bias = const.tile([P, OUT], BF16)
         nc.sync.dma_start(out=fc2_bias[:], in_=fc2_b.partition_broadcast(P))
+
+        for part in range(1, LOADS + 1):
+            if part < LOADS:
+                load(nc.gpsimd, "concat", concat_rows, part)
+            load(nc.gpsimd, "g0", g0_rows, part - 1)
 
         bias_rows_f32 = const.tile([P, P], F32)
         nc.vector.tensor_copy(out=bias_rows_f32[:], in_=bias_rows[:])
@@ -241,11 +250,6 @@ def tile_nnapprox_pa_t_kernel(
         unused = const.tile([P, OUT], F32)
 
         for turn in range(CHUNKS + DIFF_TURN):
-            if live(turn + LOAD_AHEAD):
-                load("concat", concat_rows, turn + LOAD_AHEAD)
-            if live(turn - H_TURN + LOAD_AHEAD):
-                load("g0", g0_rows, turn - H_TURN + LOAD_AHEAD)
-
             if live(turn - FC2_TURN):
                 quantise("g0", turn - FC2_TURN)
             if live(turn - DIFF_TURN):

@@ -31,11 +31,11 @@ BANKS = CHUNK_TILES // BANK_TILES
 FLOPS = 2 * ROWS * K * (OUT + HIDDEN + OUT)
 
 FC1_TURN = 1
-H_TURN = 3
-FC2_TURN = 4
-DIFF_TURN = 5
-LOAD_CHUNKS = 2
-LOADS = CHUNKS // LOAD_CHUNKS
+H_TURN = 5
+FC2_TURN = 6
+DIFF_TURN = 7
+MOVE_CHUNKS = 2
+LOAD_AHEAD = 3
 
 
 def tile_nnapprox_pa_t_kernel(
@@ -60,9 +60,9 @@ def tile_nnapprox_pa_t_kernel(
     with ExitStack() as ctx:
         ctx.enter_context(tc.manual_schedule())
         const = ctx.enter_context(tc.tile_pool(name="const", bufs=1))
-        loads = ctx.enter_context(tc.tile_pool(name="loads", bufs=LOADS))
+        loads = ctx.enter_context(tc.tile_pool(name="loads", bufs=LOAD_AHEAD + 1))
         work = ctx.enter_context(tc.tile_pool(name="work", bufs=2))
-        moved = ctx.enter_context(tc.tile_pool(name="moved", bufs=H_TURN - FC1_TURN + 1))
+        moved = ctx.enter_context(tc.tile_pool(name="moved", bufs=3))
         t_psum = ctx.enter_context(tc.psum_pool(name="t_psum", bufs=3))
         h_psum = ctx.enter_context(tc.psum_pool(name="h_psum", bufs=HIDDEN_TILES))
         d_psum = ctx.enter_context(tc.psum_pool(name="d_psum", bufs=1))
@@ -72,14 +72,11 @@ def tile_nnapprox_pa_t_kernel(
         def live(chunk):
             return 0 <= chunk < CHUNKS
 
-        def load(queue, name, rows, part):
-            x = loads.tile([P, LOAD_CHUNKS, CHUNK_TILES, K], BF16, name=name, tag=name)
-            first = part * LOAD_CHUNKS * CHUNK_TILES
-            queue.dma_start(
-                out=x[:].rearrange("p c r k -> p (c r) k"), in_=rows[:, first : first + LOAD_CHUNKS * CHUNK_TILES, :]
-            )
-            for c in range(LOAD_CHUNKS):
-                tiles[name, part * LOAD_CHUNKS + c] = x[:, c, :, :]
+        def load(name, rows, chunk):
+            x = loads.tile([P, CHUNK_TILES, K], BF16, name=name, tag=name)
+            first = chunk * CHUNK_TILES
+            nc.sync.dma_start(out=x[:], in_=rows[:, first : first + CHUNK_TILES, :])
+            tiles[name, chunk] = x
 
         def transpose(name, chunk):
             x = tiles[name, chunk]
@@ -128,21 +125,29 @@ def tile_nnapprox_pa_t_kernel(
                 )
                 tiles["h_bank", chunk, j] = bank
 
-        def silu_and_move(chunk, j):
-            if j == 0:
-                tiles["h_t", chunk] = work.tile([P, HIDDEN_TILES, CHUNK], BF16, name="h_t", tag="h_t")
-                tiles["h_planes", chunk] = moved.tile([P, PACK, CHUNK], BF16, name="h_planes", tag="h_planes")
-            h_t = tiles["h_t", chunk]
+        def silu(chunk, j):
+            pair = chunk // MOVE_CHUNKS
+            if chunk % MOVE_CHUNKS == 0 and j == 0:
+                tiles["h_t", pair] = work.tile([P, HIDDEN_TILES, MOVE_CHUNKS, CHUNK], BF16, name="h_t", tag="h_t")
             nc.scalar.activation(
-                out=h_t[:, j, :], in_=tiles["h_bank", chunk, j][:], func=ACT.Silu, bias=fc1_bias[:, j : j + 1], scale=1.0
+                out=tiles["h_t", pair][:, j, chunk % MOVE_CHUNKS, :],
+                in_=tiles["h_bank", chunk, j][:],
+                func=ACT.Silu,
+                bias=fc1_bias[:, j : j + 1],
+                scale=1.0,
             )
-            nc.sync.dma_start(out=tiles["h_planes", chunk][j:P:HIDDEN_TILES, :, :], in_=h_t[:, j, :])
+
+        def move_h(pair):
+            h_planes = moved.tile([P, PACK, MOVE_CHUNKS, CHUNK], BF16, name="h_planes", tag="h_planes")
+            for t in range(PACK):
+                nc.sync.dma_start(out=h_planes[:, t, :, :], in_=tiles["h_t", pair][t:P:PACK, :, :, :])
+            tiles["h_planes", pair] = h_planes
 
         def regroup_h(chunk):
             grouped = work.tile([P, CHUNK_TILES, P, PACK], BF16, name="h_grouped", tag="h_grouped", align_bytes=64)
             nc.vector.tensor_scalar(
                 out=grouped[:].rearrange("p r (c i) t -> p (r c) t i", i=4),
-                in0=tiles["h_planes", chunk][:].rearrange("p t (c i) -> p c t i", i=4),
+                in0=tiles["h_planes", chunk // MOVE_CHUNKS][:, :, chunk % MOVE_CHUNKS, :].rearrange("p t (c i) -> p c t i", i=4),
                 scalar1=-1.0,
                 scalar2=None,
                 op0=ALU.mult,
@@ -199,8 +204,6 @@ def tile_nnapprox_pa_t_kernel(
                     in_=scales[0, 4 * quad : 4 * quad + 4, :].bitcast(I32),
                 )
 
-        load(nc.sync, "concat", concat_rows, 0)
-
         ident = const.tile([P, P], F32)
         make_identity(nc, ident[:])
 
@@ -217,15 +220,12 @@ def tile_nnapprox_pa_t_kernel(
             in_=fc1_b.rearrange("(a j t) -> j a t", j=HIDDEN_TILES, t=PACK),
         )
         load_weight(fc1_w_words, fc1_w_scales, fc1_words_in, 0)
+        for chunk in range(LOAD_AHEAD):
+            load("concat", concat_rows, chunk)
         load_weight(w2_0_words, w2_0_scales, w2_words, HIDDEN)
         load_weight(fc2_w_words, fc2_w_scales, fc2_words, HIDDEN + OUT)
         fc2_bias = const.tile([P, OUT], BF16)
         nc.sync.dma_start(out=fc2_bias[:], in_=fc2_b.partition_broadcast(P))
-
-        for part in range(1, LOADS + 1):
-            if part < LOADS:
-                load(nc.gpsimd, "concat", concat_rows, part)
-            load(nc.gpsimd, "g0", g0_rows, part - 1)
 
         bias_rows_f32 = const.tile([P, P], F32)
         nc.vector.tensor_copy(out=bias_rows_f32[:], in_=bias_rows[:])
@@ -250,6 +250,11 @@ def tile_nnapprox_pa_t_kernel(
         unused = const.tile([P, OUT], F32)
 
         for turn in range(CHUNKS + DIFF_TURN):
+            if live(turn + LOAD_AHEAD):
+                load("concat", concat_rows, turn + LOAD_AHEAD)
+            if live(turn - H_TURN + LOAD_AHEAD):
+                load("g0", g0_rows, turn - H_TURN + LOAD_AHEAD)
+
             if live(turn - FC2_TURN):
                 quantise("g0", turn - FC2_TURN)
             if live(turn - DIFF_TURN):
@@ -273,10 +278,12 @@ def tile_nnapprox_pa_t_kernel(
                 transpose("g0", turn - H_TURN)
             for half in range(BANKS):
                 if live(turn - FC1_TURN):
-                    silu_and_move(turn - FC1_TURN, 2 * half)
-                    silu_and_move(turn - FC1_TURN, 2 * half + 1)
+                    silu(turn - FC1_TURN, 2 * half)
+                    silu(turn - FC1_TURN, 2 * half + 1)
                 if live(turn - H_TURN):
                     empty_bank(nc.scalar.copy, "g0", turn - H_TURN, half)
+            if live(turn - FC1_TURN) and (turn - FC1_TURN) % MOVE_CHUNKS == MOVE_CHUNKS - 1:
+                move_h((turn - FC1_TURN) // MOVE_CHUNKS)
 
             if live(turn - FC2_TURN):
                 fc2_minus(turn - FC2_TURN)

@@ -281,7 +281,7 @@ def tile_nnapprox_pa_t_kernel(
                     silu(turn - FC1_TURN, 2 * half)
                     silu(turn - FC1_TURN, 2 * half + 1)
                 if live(turn - H_TURN):
-                    empty_bank(nc.scalar.copy, "g0", turn - H_TURN, half)
+                    empty_bank(nc.vector.tensor_copy, "g0", turn - H_TURN, half)
             if live(turn - FC1_TURN) and (turn - FC1_TURN) % MOVE_CHUNKS == MOVE_CHUNKS - 1:
                 move_h((turn - FC1_TURN) // MOVE_CHUNKS)
 

@@ -12,6 +12,7 @@ FP8X4 = mybir.dt.float8_e4m3fn_x4
 FP4X4 = mybir.dt.float4_e2m1fn_x4
 ACT = mybir.ActivationFunctionType
 ALU = mybir.AluOpType
+AXIS = mybir.AxisListType
 
 P = 128
 PACK = 4
@@ -34,6 +35,7 @@ FC1_TURN = 1
 H_TURN = 5
 FC2_TURN = 6
 DIFF_TURN = 7
+SUM_TURN = 8
 MOVE_CHUNKS = 2
 LOAD_AHEAD = 3
 
@@ -188,12 +190,14 @@ def tile_nnapprox_pa_t_kernel(
             )
             tiles["diff", chunk] = diff
 
-        def sum_norms(chunk):
-            diff = tiles["diff", chunk]
-            for r in range(CHUNK_TILES):
-                col = chunk * CHUNK_TILES + r
-                nc.scalar.activation(out=unused[:], in_=diff[:, r, :], func=ACT.Square, accum_out=sum_sq[:, col : col + 1])
-                nc.scalar.activation(out=unused[:], in_=diff[:, r, :], func=ACT.Abs, accum_out=sum_abs[:, col : col + 1])
+        def square_and_abs(chunk):
+            terms = work.tile([P, 2, CHUNK_TILES, OUT], F32, name="terms", tag="terms")
+            nc.scalar.activation(out=terms[:, 0, :, :], in_=tiles["diff", chunk][:], func=ACT.Square)
+            nc.scalar.activation(out=terms[:, 1, :, :], in_=tiles["diff", chunk][:], func=ACT.Abs)
+            tiles["terms", chunk] = terms
+
+        def sum_terms(chunk):
+            nc.vector.tensor_reduce(out=sums[:, chunk, :, :], in_=tiles["terms", chunk][:], axis=AXIS.X, op=ALU.add)
 
         def load_weight(words, scales, words_tile, first_col):
             cols = scales.shape[2]
@@ -245,11 +249,9 @@ def tile_nnapprox_pa_t_kernel(
             in_=weight_scales[:, 0:HIDDEN].bitcast(I32).rearrange("p (a j) -> p j a", j=HIDDEN_TILES),
         )
 
-        sum_sq = const.tile([P, ROW_TILES], F32)
-        sum_abs = const.tile([P, ROW_TILES], F32)
-        unused = const.tile([P, OUT], F32)
+        sums = const.tile([P, CHUNKS, 2, CHUNK_TILES], F32)
 
-        for turn in range(CHUNKS + DIFF_TURN):
+        for turn in range(CHUNKS + SUM_TURN):
             if live(turn + LOAD_AHEAD):
                 load("concat", concat_rows, turn + LOAD_AHEAD)
             if live(turn - H_TURN + LOAD_AHEAD):
@@ -259,40 +261,41 @@ def tile_nnapprox_pa_t_kernel(
                 quantise("g0", turn - FC2_TURN)
             if live(turn - DIFF_TURN):
                 subtract_bias(turn - DIFF_TURN)
-
             if live(turn):
                 transpose("concat", turn)
-                empty_bank(nc.vector.tensor_copy, "concat", turn, 0)
-            if live(turn - H_TURN):
-                regroup_h(turn - H_TURN)
-            if live(turn):
-                empty_bank(nc.vector.tensor_copy, "concat", turn, 1)
-            if live(turn - H_TURN):
-                quantise("h", turn - H_TURN)
-            if live(turn):
-                quantise("concat", turn)
-
             if live(turn - FC1_TURN):
                 fc1(turn - FC1_TURN)
             if live(turn - H_TURN):
                 transpose("g0", turn - H_TURN)
+            if live(turn - FC2_TURN):
+                fc2_minus(turn - FC2_TURN)
+
+            if live(turn):
+                empty_bank(nc.vector.tensor_copy, "concat", turn, 0)
+                empty_bank(nc.scalar.copy, "concat", turn, 1)
             for half in range(BANKS):
                 if live(turn - FC1_TURN):
                     silu(turn - FC1_TURN, 2 * half)
                     silu(turn - FC1_TURN, 2 * half + 1)
                 if live(turn - H_TURN):
-                    empty_bank(nc.vector.tensor_copy, "g0", turn - H_TURN, half)
+                    empty_bank(nc.scalar.copy, "g0", turn - H_TURN, half)
             if live(turn - FC1_TURN) and (turn - FC1_TURN) % MOVE_CHUNKS == MOVE_CHUNKS - 1:
                 move_h((turn - FC1_TURN) // MOVE_CHUNKS)
-
-            if live(turn - FC2_TURN):
-                fc2_minus(turn - FC2_TURN)
             if live(turn - DIFF_TURN):
-                sum_norms(turn - DIFF_TURN)
+                square_and_abs(turn - DIFF_TURN)
 
-        l2 = const.tile([P, ROW_TILES], F32)
-        nc.scalar.activation(out=l2[:], in_=sum_sq[:], func=ACT.Sqrt)
-        l1 = const.tile([P, ROW_TILES], F32)
-        nc.vector.tensor_scalar(out=l1[:], in0=sum_abs[:], scalar1=1.0 / OUT, scalar2=None, op0=ALU.mult)
-        nc.sync.dma_start(out=out_0.rearrange("(p r) -> p r", r=ROW_TILES), in_=l2[:])
-        nc.sync.dma_start(out=out_1.rearrange("(p r) -> p r", r=ROW_TILES), in_=l1[:])
+            if live(turn - H_TURN):
+                regroup_h(turn - H_TURN)
+            if live(turn - SUM_TURN):
+                sum_terms(turn - SUM_TURN)
+            if live(turn - H_TURN):
+                quantise("h", turn - H_TURN)
+            if live(turn):
+                quantise("concat", turn)
+
+        l2 = const.tile([P, CHUNKS, CHUNK_TILES], F32)
+        nc.scalar.activation(out=l2[:], in_=sums[:, :, 0, :], func=ACT.Sqrt)
+        l1 = const.tile([P, CHUNKS, CHUNK_TILES], F32)
+        nc.vector.tensor_scalar(out=l1[:], in0=sums[:, :, 1, :], scalar1=1.0 / OUT, scalar2=None, op0=ALU.mult)
+        nc.sync.dma_start(out=out_0.rearrange("(p r) -> p r", r=ROW_TILES), in_=l2[:].rearrange("p c r -> p (c r)"))
+        nc.sync.dma_start(out=out_1.rearrange("(p r) -> p r", r=ROW_TILES), in_=l1[:].rearrange("p c r -> p (c r)"))

@@ -12,7 +12,6 @@ FP8X4 = mybir.dt.float8_e4m3fn_x4
 FP4X4 = mybir.dt.float4_e2m1fn_x4
 ACT = mybir.ActivationFunctionType
 ALU = mybir.AluOpType
-AXIS = mybir.AxisListType
 
 P = 128
 PACK = 4
@@ -35,7 +34,6 @@ FC1_TURN = 1
 H_TURN = 5
 FC2_TURN = 6
 DIFF_TURN = 7
-SUM_TURN = 8
 MOVE_CHUNKS = 2
 LOAD_AHEAD = 3
 
@@ -190,14 +188,13 @@ def tile_nnapprox_pa_t_kernel(
             )
             tiles["diff", chunk] = diff
 
-        def square_and_abs(chunk):
+        def sum_norms(chunk):
+            diff = tiles["diff", chunk]
             terms = work.tile([P, 2, CHUNK_TILES, OUT], F32, name="terms", tag="terms")
-            nc.scalar.activation(out=terms[:, 0, :, :], in_=tiles["diff", chunk][:], func=ACT.Square)
-            nc.scalar.activation(out=terms[:, 1, :, :], in_=tiles["diff", chunk][:], func=ACT.Abs)
-            tiles["terms", chunk] = terms
-
-        def sum_terms(chunk):
-            nc.vector.tensor_reduce(out=sums[:, chunk, :, :], in_=tiles["terms", chunk][:], axis=AXIS.X, op=ALU.add)
+            for r in range(CHUNK_TILES):
+                col = chunk * CHUNK_TILES + r
+                nc.scalar.activation(out=terms[:, 0, r, :], in_=diff[:, r, :], func=ACT.Square, accum_out=sum_sq[:, col : col + 1])
+                nc.scalar.activation(out=terms[:, 1, r, :], in_=diff[:, r, :], func=ACT.Abs, accum_out=sum_abs[:, col : col + 1])
 
         def load_weight(words, scales, words_tile, first_col):
             cols = scales.shape[2]
@@ -249,9 +246,10 @@ def tile_nnapprox_pa_t_kernel(
             in_=weight_scales[:, 0:HIDDEN].bitcast(I32).rearrange("p (a j) -> p j a", j=HIDDEN_TILES),
         )
 
-        sums = const.tile([P, CHUNKS, 2, CHUNK_TILES], F32)
+        sum_sq = const.tile([P, ROW_TILES], F32)
+        sum_abs = const.tile([P, ROW_TILES], F32)
 
-        for turn in range(CHUNKS + SUM_TURN):
+        for turn in range(CHUNKS + DIFF_TURN):
             if live(turn + LOAD_AHEAD):
                 load("concat", concat_rows, turn + LOAD_AHEAD)
             if live(turn - H_TURN + LOAD_AHEAD):
@@ -261,18 +259,23 @@ def tile_nnapprox_pa_t_kernel(
                 quantise("g0", turn - FC2_TURN)
             if live(turn - DIFF_TURN):
                 subtract_bias(turn - DIFF_TURN)
+
             if live(turn):
                 transpose("concat", turn)
+                empty_bank(nc.vector.tensor_copy, "concat", turn, 0)
+            if live(turn - H_TURN):
+                regroup_h(turn - H_TURN)
+            if live(turn):
+                empty_bank(nc.vector.tensor_copy, "concat", turn, 1)
+            if live(turn - H_TURN):
+                quantise("h", turn - H_TURN)
+            if live(turn):
+                quantise("concat", turn)
+
             if live(turn - FC1_TURN):
                 fc1(turn - FC1_TURN)
             if live(turn - H_TURN):
                 transpose("g0", turn - H_TURN)
-            if live(turn - FC2_TURN):
-                fc2_minus(turn - FC2_TURN)
-
-            if live(turn):
-                empty_bank(nc.vector.tensor_copy, "concat", turn, 0)
-                empty_bank(nc.scalar.copy, "concat", turn, 1)
             for half in range(BANKS):
                 if live(turn - FC1_TURN):
                     silu(turn - FC1_TURN, 2 * half)
@@ -281,21 +284,15 @@ def tile_nnapprox_pa_t_kernel(
                     empty_bank(nc.scalar.copy, "g0", turn - H_TURN, half)
             if live(turn - FC1_TURN) and (turn - FC1_TURN) % MOVE_CHUNKS == MOVE_CHUNKS - 1:
                 move_h((turn - FC1_TURN) // MOVE_CHUNKS)
+
+            if live(turn - FC2_TURN):
+                fc2_minus(turn - FC2_TURN)
             if live(turn - DIFF_TURN):
-                square_and_abs(turn - DIFF_TURN)
+                sum_norms(turn - DIFF_TURN)
 
-            if live(turn - H_TURN):
-                regroup_h(turn - H_TURN)
-            if live(turn - SUM_TURN):
-                sum_terms(turn - SUM_TURN)
-            if live(turn - H_TURN):
-                quantise("h", turn - H_TURN)
-            if live(turn):
-                quantise("concat", turn)
-
-        l2 = const.tile([P, CHUNKS, CHUNK_TILES], F32)
-        nc.scalar.activation(out=l2[:], in_=sums[:, :, 0, :], func=ACT.Sqrt)
-        l1 = const.tile([P, CHUNKS, CHUNK_TILES], F32)
-        nc.vector.tensor_scalar(out=l1[:], in0=sums[:, :, 1, :], scalar1=1.0 / OUT, scalar2=None, op0=ALU.mult)
-        nc.sync.dma_start(out=out_0.rearrange("(p r) -> p r", r=ROW_TILES), in_=l2[:].rearrange("p c r -> p (c r)"))
-        nc.sync.dma_start(out=out_1.rearrange("(p r) -> p r", r=ROW_TILES), in_=l1[:].rearrange("p c r -> p (c r)"))
+        l2 = const.tile([P, ROW_TILES], F32)
+        nc.scalar.activation(out=l2[:], in_=sum_sq[:], func=ACT.Sqrt)
+        l1 = const.tile([P, ROW_TILES], F32)
+        nc.vector.tensor_scalar(out=l1[:], in0=sum_abs[:], scalar1=1.0 / OUT, scalar2=None, op0=ALU.mult)
+        nc.sync.dma_start(out=out_0.rearrange("(p r) -> p r", r=ROW_TILES), in_=l2[:])
+        nc.sync.dma_start(out=out_1.rearrange("(p r) -> p r", r=ROW_TILES), in_=l1[:])

@@ -31,10 +31,9 @@ BANKS = CHUNK_TILES // BANK_TILES
 FLOPS = 2 * ROWS * K * (OUT + HIDDEN + OUT)
 
 FC1_TURN = 1
-H_TURN = 5
-FC2_TURN = 6
-DIFF_TURN = 7
-MOVE_CHUNKS = 2
+H_TURN = 2
+FC2_TURN = 3
+DIFF_TURN = 4
 LOAD_AHEAD = 3
 
 
@@ -62,7 +61,6 @@ def tile_nnapprox_pa_t_kernel(
         const = ctx.enter_context(tc.tile_pool(name="const", bufs=1))
         loads = ctx.enter_context(tc.tile_pool(name="loads", bufs=LOAD_AHEAD + 1))
         work = ctx.enter_context(tc.tile_pool(name="work", bufs=2))
-        moved = ctx.enter_context(tc.tile_pool(name="moved", bufs=3))
         t_psum = ctx.enter_context(tc.psum_pool(name="t_psum", bufs=3))
         h_psum = ctx.enter_context(tc.psum_pool(name="h_psum", bufs=HIDDEN_TILES))
         d_psum = ctx.enter_context(tc.psum_pool(name="d_psum", bufs=1))
@@ -126,28 +124,21 @@ def tile_nnapprox_pa_t_kernel(
                 tiles["h_bank", chunk, j] = bank
 
         def silu(chunk, j):
-            pair = chunk // MOVE_CHUNKS
-            if chunk % MOVE_CHUNKS == 0 and j == 0:
-                tiles["h_t", pair] = work.tile([P, HIDDEN_TILES, MOVE_CHUNKS, CHUNK], BF16, name="h_t", tag="h_t")
+            if j == 0:
+                tiles["h_t", chunk] = work.tile([P, PACK, CHUNK], BF16, name="h_t", tag="h_t")
             nc.scalar.activation(
-                out=tiles["h_t", pair][:, j, chunk % MOVE_CHUNKS, :],
+                out=tiles["h_t", chunk][:, j, :],
                 in_=tiles["h_bank", chunk, j][:],
                 func=ACT.Silu,
                 bias=fc1_bias[:, j : j + 1],
                 scale=1.0,
             )
 
-        def move_h(pair):
-            h_planes = moved.tile([P, PACK, MOVE_CHUNKS, CHUNK], BF16, name="h_planes", tag="h_planes")
-            for t in range(PACK):
-                nc.sync.dma_start(out=h_planes[:, t, :, :], in_=tiles["h_t", pair][t:P:PACK, :, :, :])
-            tiles["h_planes", pair] = h_planes
-
         def regroup_h(chunk):
             grouped = work.tile([P, CHUNK_TILES, P, PACK], BF16, name="h_grouped", tag="h_grouped", align_bytes=64)
             nc.vector.tensor_scalar(
                 out=grouped[:].rearrange("p r (c i) t -> p (r c) t i", i=4),
-                in0=tiles["h_planes", chunk // MOVE_CHUNKS][:, :, chunk % MOVE_CHUNKS, :].rearrange("p t (c i) -> p c t i", i=4),
+                in0=tiles["h_t", chunk][:].rearrange("p t (c i) -> p c t i", i=4),
                 scalar1=-1.0,
                 scalar2=None,
                 op0=ALU.mult,
@@ -214,36 +205,27 @@ def tile_nnapprox_pa_t_kernel(
         w2_words = const.tile([P, 2 * OUT], U8, align_bytes=64)
         fc2_words = const.tile([P, 2 * OUT], U8, align_bytes=64)
 
-        bias_rows = const.tile([P, P], BF16)
-        nc.vector.memset(bias_rows[:], 0.0)
-        nc.sync.dma_start(
-            out=bias_rows[0:HIDDEN_TILES, :].rearrange("j (a t) -> j a t", t=PACK),
-            in_=fc1_b.rearrange("(a j t) -> j a t", j=HIDDEN_TILES, t=PACK),
-        )
+        fc1_bias = const.tile([P, PACK], BF16)
+        nc.sync.dma_start(out=fc1_bias[:], in_=fc1_b.rearrange("(p t) -> p t", t=PACK))
         load_weight(fc1_w_words, fc1_w_scales, fc1_words_in, 0)
         for chunk in range(LOAD_AHEAD):
             load("concat", concat_rows, chunk)
         load_weight(w2_0_words, w2_0_scales, w2_words, HIDDEN)
         load_weight(fc2_w_words, fc2_w_scales, fc2_words, HIDDEN + OUT)
+        for chunk in range(LOAD_AHEAD - H_TURN):
+            load("g0", g0_rows, chunk)
         fc2_bias = const.tile([P, OUT], BF16)
         nc.sync.dma_start(out=fc2_bias[:], in_=fc2_b.partition_broadcast(P))
 
-        bias_rows_f32 = const.tile([P, P], F32)
-        nc.vector.tensor_copy(out=bias_rows_f32[:], in_=bias_rows[:])
-        bias_bank = t_psum.tile([P, BANK_TILES, 2, P], F32, name="t_bank", tag="t_bank")
-        nc.tensor.transpose(bias_bank[:, 0, 0, :], bias_rows_f32[:], ident[:])
-        fc1_bias = const.tile([P, HIDDEN_TILES], F32)
-        nc.vector.tensor_copy(out=fc1_bias[:], in_=bias_bank[:, 0, 0, 0:HIDDEN_TILES])
-
         fc1_words = const.tile([P, 2 * HIDDEN], U8, align_bytes=64)
         nc.vector.tensor_copy(
-            out=fc1_words[:].bitcast(I32).rearrange("p (j a w) -> p j a w", j=HIDDEN_TILES, w=2),
-            in_=fc1_words_in[:].bitcast(I32).rearrange("p (a j w) -> p j a w", j=HIDDEN_TILES, w=2),
+            out=fc1_words[:].rearrange("p (t m e) -> p t m e", t=PACK, e=2),
+            in_=fc1_words_in[:].rearrange("p (m t e) -> p t m e", t=PACK, e=2),
         )
         fc1_scales = const.tile([P, HIDDEN], U8, align_bytes=64)
         nc.vector.tensor_copy(
-            out=fc1_scales[:].bitcast(I32).rearrange("p (j a) -> p j a", j=HIDDEN_TILES),
-            in_=weight_scales[:, 0:HIDDEN].bitcast(I32).rearrange("p (a j) -> p j a", j=HIDDEN_TILES),
+            out=fc1_scales[:].rearrange("p (t m) -> p t m", t=PACK),
+            in_=weight_scales[:, 0:HIDDEN].rearrange("p (m t) -> p t m", t=PACK),
         )
 
         sum_sq = const.tile([P, ROW_TILES], F32)
@@ -282,8 +264,6 @@ def tile_nnapprox_pa_t_kernel(
                     silu(turn - FC1_TURN, 2 * half + 1)
                 if live(turn - H_TURN):
                     empty_bank(nc.scalar.copy, "g0", turn - H_TURN, half)
-            if live(turn - FC1_TURN) and (turn - FC1_TURN) % MOVE_CHUNKS == MOVE_CHUNKS - 1:
-                move_h((turn - FC1_TURN) // MOVE_CHUNKS)
 
             if live(turn - FC2_TURN):
                 fc2_minus(turn - FC2_TURN)

@@ -23,17 +23,19 @@ ROW_TILES = ROWS // P
 CHUNK_TILES = 4
 CHUNK = CHUNK_TILES * P
 CHUNKS = ROW_TILES // CHUNK_TILES
-HIDDEN_TILES = HIDDEN // P
 WORDS = K // 2
 BANK_TILES = 2
 BANKS = CHUNK_TILES // BANK_TILES
+PARITIES = 2
+STATS = 3
 
 FLOPS = 2 * ROWS * K * (OUT + HIDDEN + OUT)
 
 FC1_TURN = 1
 H_TURN = 2
 FC2_TURN = 3
-DIFF_TURN = 4
+NORM_TURN = 4
+DONE_EARLY = (CHUNKS - 2) * CHUNK_TILES
 LOAD_AHEAD = 3
 
 
@@ -60,9 +62,9 @@ def tile_nnapprox_pa_t_kernel(
         ctx.enter_context(tc.manual_schedule())
         const = ctx.enter_context(tc.tile_pool(name="const", bufs=1))
         loads = ctx.enter_context(tc.tile_pool(name="loads", bufs=LOAD_AHEAD + 1))
-        work = ctx.enter_context(tc.tile_pool(name="work", bufs=2))
-        t_psum = ctx.enter_context(tc.psum_pool(name="t_psum", bufs=3))
-        h_psum = ctx.enter_context(tc.psum_pool(name="h_psum", bufs=HIDDEN_TILES))
+        work = ctx.enter_context(tc.tile_pool(name="work", bufs=3))
+        t_psum = ctx.enter_context(tc.psum_pool(name="t_psum", bufs=4))
+        h_psum = ctx.enter_context(tc.psum_pool(name="h_psum", bufs=3))
         d_psum = ctx.enter_context(tc.psum_pool(name="d_psum", bufs=1))
 
         tiles = {}
@@ -109,28 +111,31 @@ def tile_nnapprox_pa_t_kernel(
             tiles[name + "_codes", chunk] = codes
             tiles[name + "_scales", chunk] = scales
 
-        def fc1(chunk):
-            for j in range(HIDDEN_TILES):
-                bank = h_psum.tile([P, CHUNK], F32, name="h_bank", tag="h_bank")
-                nc.tensor.matmul_mx(
-                    out=bank[:],
-                    lhsT=fc1_words[:, 2 * P * j : 2 * P * (j + 1)].bitcast(FP4X4),
-                    lhsT_scale=fc1_scales[:, P * j : P * (j + 1)],
-                    rhs=tiles["concat_codes", chunk][:].bitcast(FP8X4),
-                    rhs_scale=tiles["concat_scales", chunk][:],
-                    start=True,
-                    stop=True,
-                )
-                tiles["h_bank", chunk, j] = bank
+        def pass_mx(bank, words, scales, name, chunk, start, stop):
+            nc.tensor.matmul_mx(
+                out=bank[:],
+                lhsT=words.bitcast(FP4X4),
+                lhsT_scale=scales,
+                rhs=tiles[name + "_codes", chunk][:].bitcast(FP8X4),
+                rhs_scale=tiles[name + "_scales", chunk][:],
+                start=start,
+                stop=stop,
+            )
 
-        def silu(chunk, j):
-            if j == 0:
+        def fc1(chunk, t):
+            bank = h_psum.tile([P, CHUNK], F32, name="h_bank", tag="h_bank")
+            words = fc1_words[:, 2 * P * t : 2 * P * (t + 1)]
+            pass_mx(bank, words, fc1_scales[:, P * t : P * (t + 1)], "concat", chunk, True, True)
+            tiles["h_bank", chunk, t] = bank
+
+        def silu(chunk, t):
+            if t == 0:
                 tiles["h_t", chunk] = work.tile([P, PACK, CHUNK], BF16, name="h_t", tag="h_t")
             nc.scalar.activation(
-                out=tiles["h_t", chunk][:, j, :],
-                in_=tiles["h_bank", chunk, j][:],
+                out=tiles["h_t", chunk][:, t, :],
+                in_=tiles["h_bank", chunk, t][:],
                 func=ACT.Silu,
-                bias=fc1_bias[:, j : j + 1],
+                bias=fc1_bias[:, t : t + 1],
                 scale=1.0,
             )
 
@@ -146,46 +151,50 @@ def tile_nnapprox_pa_t_kernel(
             tiles["h_grouped", chunk] = grouped
 
         def fc2_minus(chunk):
-            bank = d_psum.tile([P, CHUNK_TILES, OUT], F32, name="d_bank", tag="d_bank")
-            for r in range(CHUNK_TILES):
-                cols = slice(r * P, (r + 1) * P)
-                nc.tensor.matmul_mx(
-                    out=bank[:, r, :],
-                    lhsT=tiles["g0_codes", chunk][:, cols].bitcast(FP8X4),
-                    lhsT_scale=tiles["g0_scales", chunk][:, cols],
-                    rhs=w2_words[:].bitcast(FP4X4),
-                    rhs_scale=weight_scales[:, HIDDEN : HIDDEN + OUT],
-                    start=True,
-                    stop=False,
-                )
-                nc.tensor.matmul_mx(
-                    out=bank[:, r, :],
-                    lhsT=tiles["h_codes", chunk][:, cols].bitcast(FP8X4),
-                    lhsT_scale=tiles["h_scales", chunk][:, cols],
-                    rhs=fc2_words[:].bitcast(FP4X4),
-                    rhs_scale=weight_scales[:, HIDDEN + OUT : HIDDEN + 2 * OUT],
-                    start=False,
-                    stop=True,
-                )
+            bank = d_psum.tile([P, CHUNK], F32, name="d_bank", tag="d_bank")
+            pass_mx(bank, w2_words[:], weight_scales[:, HIDDEN : HIDDEN + OUT], "g0", chunk, True, False)
+            pass_mx(bank, fc2_words[:], weight_scales[:, HIDDEN + OUT : HIDDEN + 2 * OUT], "h", chunk, False, True)
             tiles["d_bank", chunk] = bank
 
-        def subtract_bias(chunk):
-            diff = work.tile([P, CHUNK_TILES, OUT], F32, name="diff", tag="diff")
-            nc.vector.tensor_tensor(
-                out=diff[:],
-                in0=tiles["d_bank", chunk][:],
-                in1=fc2_bias[:].unsqueeze(1).to_broadcast([P, CHUNK_TILES, OUT]),
-                op=ALU.subtract,
+        def absolute(chunk):
+            magnitude = work.tile([P, CHUNK_TILES, P], F32, name="magnitude", tag="magnitude")
+            nc.scalar.activation(
+                out=magnitude[:].rearrange("p r b -> p (r b)"),
+                in_=tiles["d_bank", chunk][:],
+                func=ACT.Abs,
+                bias=fc2_bias[:],
+                scale=-1.0,
             )
-            tiles["diff", chunk] = diff
+            tiles["magnitude", chunk] = magnitude
 
-        def sum_norms(chunk):
-            diff = tiles["diff", chunk]
-            terms = work.tile([P, 2, CHUNK_TILES, OUT], F32, name="terms", tag="terms")
+        def transpose_back(chunk):
+            bank = t_psum.tile([P, CHUNK_TILES, OUT], F32, name="t_bank", tag="t_bank")
             for r in range(CHUNK_TILES):
-                col = chunk * CHUNK_TILES + r
-                nc.scalar.activation(out=terms[:, 0, r, :], in_=diff[:, r, :], func=ACT.Square, accum_out=sum_sq[:, col : col + 1])
-                nc.scalar.activation(out=terms[:, 1, r, :], in_=diff[:, r, :], func=ACT.Abs, accum_out=sum_abs[:, col : col + 1])
+                nc.tensor.transpose(bank[:, r, :], tiles["magnitude", chunk][:, r, :], ident[:])
+            tiles["m_bank", chunk] = bank
+
+        def row_stats(chunk):
+            for r in range(CHUNK_TILES):
+                nc.vector.bn_stats(
+                    out=stats[:, chunk * CHUNK_TILES + r, :, :].rearrange("p e s -> p (e s)"),
+                    in_=tiles["m_bank", chunk][:, r, :],
+                )
+
+        def finish(first, last):
+            n = OUT // PARITIES
+            size = last - first
+            mean = stats[:, first:last, :, 1]
+            deviation = stats[:, first:last, :, 2]
+            squares = work.tile([P, size, PARITIES], F32, name="squares", tag="squares")
+            nc.vector.tensor_tensor(out=squares[:], in0=mean, in1=mean, op=ALU.mult)
+            means = work.tile([P, size], F32, name="means", tag="means")
+            nc.vector.tensor_tensor(out=means[:], in0=mean[:, :, 0], in1=mean[:, :, 1], op=ALU.add)
+            sums = work.tile([P, size, PARITIES], F32, name="sums", tag="sums")
+            nc.vector.scalar_tensor_tensor(out=sums[:], in0=squares[:], scalar=float(n), in1=deviation, op0=ALU.mult, op1=ALU.add)
+            nc.vector.tensor_scalar(out=l1[:, first:last], in0=means[:], scalar1=n / OUT, scalar2=None, op0=ALU.mult)
+            total = work.tile([P, size], F32, name="total", tag="total")
+            nc.vector.tensor_tensor(out=total[:], in0=sums[:, :, 0], in1=sums[:, :, 1], op=ALU.add)
+            nc.scalar.activation(out=l2[:, first:last], in_=total[:], func=ACT.Sqrt)
 
         def load_weight(words, scales, words_tile, first_col):
             cols = scales.shape[2]
@@ -205,17 +214,18 @@ def tile_nnapprox_pa_t_kernel(
         w2_words = const.tile([P, 2 * OUT], U8, align_bytes=64)
         fc2_words = const.tile([P, 2 * OUT], U8, align_bytes=64)
 
+        load("concat", concat_rows, 0)
+        load_weight(fc1_w_words, fc1_w_scales, fc1_words_in, 0)
         fc1_bias = const.tile([P, PACK], BF16)
         nc.sync.dma_start(out=fc1_bias[:], in_=fc1_b.rearrange("(p t) -> p t", t=PACK))
-        load_weight(fc1_w_words, fc1_w_scales, fc1_words_in, 0)
-        for chunk in range(LOAD_AHEAD):
-            load("concat", concat_rows, chunk)
+        load("concat", concat_rows, 1)
+        load("g0", g0_rows, 0)
         load_weight(w2_0_words, w2_0_scales, w2_words, HIDDEN)
         load_weight(fc2_w_words, fc2_w_scales, fc2_words, HIDDEN + OUT)
-        for chunk in range(LOAD_AHEAD - H_TURN):
-            load("g0", g0_rows, chunk)
-        fc2_bias = const.tile([P, OUT], BF16)
-        nc.sync.dma_start(out=fc2_bias[:], in_=fc2_b.partition_broadcast(P))
+        fc2_bias = const.tile([P, 1], BF16)
+        nc.sync.dma_start(out=fc2_bias[:], in_=fc2_b.rearrange("(p o) -> p o", o=1))
+        load("concat", concat_rows, 2)
+        load("g0", g0_rows, 1)
 
         fc1_words = const.tile([P, 2 * HIDDEN], U8, align_bytes=64)
         nc.vector.tensor_copy(
@@ -228,51 +238,51 @@ def tile_nnapprox_pa_t_kernel(
             in_=weight_scales[:, 0:HIDDEN].rearrange("p (m t) -> p t m", t=PACK),
         )
 
-        sum_sq = const.tile([P, ROW_TILES], F32)
-        sum_abs = const.tile([P, ROW_TILES], F32)
+        stats = const.tile([P, ROW_TILES, PARITIES, STATS], F32)
+        l2 = const.tile([P, ROW_TILES], F32)
+        l1 = const.tile([P, ROW_TILES], F32)
 
-        for turn in range(CHUNKS + DIFF_TURN):
+        for turn in range(CHUNKS + NORM_TURN):
             if live(turn + LOAD_AHEAD):
                 load("concat", concat_rows, turn + LOAD_AHEAD)
-            if live(turn - H_TURN + LOAD_AHEAD):
-                load("g0", g0_rows, turn - H_TURN + LOAD_AHEAD)
-
-            if live(turn - FC2_TURN):
-                quantise("g0", turn - FC2_TURN)
-            if live(turn - DIFF_TURN):
-                subtract_bias(turn - DIFF_TURN)
+            if live(turn - FC1_TURN + LOAD_AHEAD):
+                load("g0", g0_rows, turn - FC1_TURN + LOAD_AHEAD)
 
             if live(turn):
                 transpose("concat", turn)
+            if live(turn - FC1_TURN):
+                transpose("g0", turn - FC1_TURN)
+            if live(turn - NORM_TURN):
+                absolute(turn - NORM_TURN)
+                transpose_back(turn - NORM_TURN)
+
+            if live(turn - H_TURN):
+                quantise("g0", turn - H_TURN)
+            if live(turn):
                 empty_bank(nc.vector.tensor_copy, "concat", turn, 0)
+                empty_bank(nc.scalar.copy, "concat", turn, 1)
             if live(turn - H_TURN):
                 regroup_h(turn - H_TURN)
-            if live(turn):
-                empty_bank(nc.vector.tensor_copy, "concat", turn, 1)
-            if live(turn - H_TURN):
-                quantise("h", turn - H_TURN)
+            if live(turn - FC1_TURN):
+                empty_bank(nc.scalar.copy, "g0", turn - FC1_TURN, 0)
+                empty_bank(nc.scalar.copy, "g0", turn - FC1_TURN, 1)
             if live(turn):
                 quantise("concat", turn)
-
-            if live(turn - FC1_TURN):
-                fc1(turn - FC1_TURN)
+            if live(turn - NORM_TURN):
+                row_stats(turn - NORM_TURN)
             if live(turn - H_TURN):
-                transpose("g0", turn - H_TURN)
-            for half in range(BANKS):
+                quantise("h", turn - H_TURN)
+
+            for t in range(PACK):
+                if t == PACK // 2 and live(turn - FC2_TURN):
+                    fc2_minus(turn - FC2_TURN)
                 if live(turn - FC1_TURN):
-                    silu(turn - FC1_TURN, 2 * half)
-                    silu(turn - FC1_TURN, 2 * half + 1)
-                if live(turn - H_TURN):
-                    empty_bank(nc.scalar.copy, "g0", turn - H_TURN, half)
+                    fc1(turn - FC1_TURN, t)
+                    silu(turn - FC1_TURN, t)
 
-            if live(turn - FC2_TURN):
-                fc2_minus(turn - FC2_TURN)
-            if live(turn - DIFF_TURN):
-                sum_norms(turn - DIFF_TURN)
+            if turn == CHUNKS + FC2_TURN - 1:
+                finish(0, DONE_EARLY)
 
-        l2 = const.tile([P, ROW_TILES], F32)
-        nc.scalar.activation(out=l2[:], in_=sum_sq[:], func=ACT.Sqrt)
-        l1 = const.tile([P, ROW_TILES], F32)
-        nc.vector.tensor_scalar(out=l1[:], in0=sum_abs[:], scalar1=1.0 / OUT, scalar2=None, op0=ALU.mult)
-        nc.sync.dma_start(out=out_0.rearrange("(p r) -> p r", r=ROW_TILES), in_=l2[:])
+        finish(DONE_EARLY, ROW_TILES)
         nc.sync.dma_start(out=out_1.rearrange("(p r) -> p r", r=ROW_TILES), in_=l1[:])
+        nc.sync.dma_start(out=out_0.rearrange("(p r) -> p r", r=ROW_TILES), in_=l2[:])

@@ -34,8 +34,9 @@ FLOPS = 2 * ROWS * K * (OUT + HIDDEN + OUT)
 FC1_TURN = 1
 H_TURN = 2
 FC2_TURN = 3
-NORM_TURN = 4
-DONE_EARLY = (CHUNKS - 2) * CHUNK_TILES
+ABS_TURN = 4
+NORM_TURN = 5
+DONE_EARLY = (CHUNKS - 3) * CHUNK_TILES
 LOAD_AHEAD = 3
 
 
@@ -214,18 +215,24 @@ def tile_nnapprox_pa_t_kernel(
         w2_words = const.tile([P, 2 * OUT], U8, align_bytes=64)
         fc2_words = const.tile([P, 2 * OUT], U8, align_bytes=64)
 
-        load("concat", concat_rows, 0)
+        first_chunk = loads.tile([P, CHUNK_TILES, K], BF16, name="concat", tag="concat")
+        for half in range(BANKS):
+            row_tiles = slice(half * BANK_TILES, (half + 1) * BANK_TILES)
+            nc.sync.dma_start(out=first_chunk[:, row_tiles, :], in_=concat_rows[:, row_tiles, :])
+        tiles["concat", 0] = first_chunk
         load_weight(fc1_w_words, fc1_w_scales, fc1_words_in, 0)
         fc1_bias = const.tile([P, PACK], BF16)
         nc.sync.dma_start(out=fc1_bias[:], in_=fc1_b.rearrange("(p t) -> p t", t=PACK))
         load("concat", concat_rows, 1)
-        load("g0", g0_rows, 0)
         load_weight(w2_0_words, w2_0_scales, w2_words, HIDDEN)
         load_weight(fc2_w_words, fc2_w_scales, fc2_words, HIDDEN + OUT)
         fc2_bias = const.tile([P, 1], BF16)
         nc.sync.dma_start(out=fc2_bias[:], in_=fc2_b.rearrange("(p o) -> p o", o=1))
         load("concat", concat_rows, 2)
-        load("g0", g0_rows, 1)
+        load("g0", g0_rows, 0)
+
+        unread = const.tile([P, 1], F32)
+        nc.scalar.activation(out=unread[:], in_=ident[:, 0:1], func=ACT.Silu)
 
         fc1_words = const.tile([P, 2 * HIDDEN], U8, align_bytes=64)
         nc.vector.tensor_copy(
@@ -245,33 +252,32 @@ def tile_nnapprox_pa_t_kernel(
         for turn in range(CHUNKS + NORM_TURN):
             if live(turn + LOAD_AHEAD):
                 load("concat", concat_rows, turn + LOAD_AHEAD)
-            if live(turn - FC1_TURN + LOAD_AHEAD):
-                load("g0", g0_rows, turn - FC1_TURN + LOAD_AHEAD)
+            if live(turn - H_TURN + LOAD_AHEAD):
+                load("g0", g0_rows, turn - H_TURN + LOAD_AHEAD)
 
             if live(turn):
                 transpose("concat", turn)
-            if live(turn - FC1_TURN):
-                transpose("g0", turn - FC1_TURN)
+            if live(turn - H_TURN):
+                transpose("g0", turn - H_TURN)
             if live(turn - NORM_TURN):
-                absolute(turn - NORM_TURN)
                 transpose_back(turn - NORM_TURN)
 
-            if live(turn - H_TURN):
-                quantise("g0", turn - H_TURN)
+            if live(turn - ABS_TURN):
+                absolute(turn - ABS_TURN)
             if live(turn):
                 empty_bank(nc.vector.tensor_copy, "concat", turn, 0)
-                empty_bank(nc.scalar.copy, "concat", turn, 1)
+                empty_bank(nc.vector.tensor_copy if turn % 2 == 0 else nc.scalar.copy, "concat", turn, 1)
             if live(turn - H_TURN):
+                empty_bank(nc.scalar.copy, "g0", turn - H_TURN, 0)
+                empty_bank(nc.scalar.copy, "g0", turn - H_TURN, 1)
                 regroup_h(turn - H_TURN)
-            if live(turn - FC1_TURN):
-                empty_bank(nc.scalar.copy, "g0", turn - FC1_TURN, 0)
-                empty_bank(nc.scalar.copy, "g0", turn - FC1_TURN, 1)
             if live(turn):
                 quantise("concat", turn)
             if live(turn - NORM_TURN):
                 row_stats(turn - NORM_TURN)
             if live(turn - H_TURN):
                 quantise("h", turn - H_TURN)
+                quantise("g0", turn - H_TURN)
 
             for t in range(PACK):
                 if t == PACK // 2 and live(turn - FC2_TURN):
@@ -280,7 +286,7 @@ def tile_nnapprox_pa_t_kernel(
                     fc1(turn - FC1_TURN, t)
                     silu(turn - FC1_TURN, t)
 
-            if turn == CHUNKS + FC2_TURN - 1:
+            if turn == CHUNKS + FC1_TURN:
                 finish(0, DONE_EARLY)
 
         finish(DONE_EARLY, ROW_TILES)

@@ -64,8 +64,8 @@ def tile_nnapprox_pa_t_kernel(
         const = ctx.enter_context(tc.tile_pool(name="const", bufs=1))
         loads = ctx.enter_context(tc.tile_pool(name="loads", bufs=LOAD_AHEAD + 1))
         work = ctx.enter_context(tc.tile_pool(name="work", bufs=3))
-        t_psum = ctx.enter_context(tc.psum_pool(name="t_psum", bufs=4))
-        h_psum = ctx.enter_context(tc.psum_pool(name="h_psum", bufs=3))
+        t_psum = ctx.enter_context(tc.psum_pool(name="t_psum", bufs=3))
+        h_psum = ctx.enter_context(tc.psum_pool(name="h_psum", bufs=PACK))
         d_psum = ctx.enter_context(tc.psum_pool(name="d_psum", bufs=1))
 
         tiles = {}
@@ -257,6 +257,9 @@ def tile_nnapprox_pa_t_kernel(
 
             if live(turn):
                 transpose("concat", turn)
+            if live(turn - FC1_TURN):
+                for t in range(PACK):
+                    fc1(turn - FC1_TURN, t)
             if live(turn - H_TURN):
                 transpose("g0", turn - H_TURN)
             if live(turn - NORM_TURN):
@@ -267,9 +270,14 @@ def tile_nnapprox_pa_t_kernel(
             if live(turn):
                 empty_bank(nc.vector.tensor_copy, "concat", turn, 0)
                 empty_bank(nc.vector.tensor_copy if turn % 2 == 0 else nc.scalar.copy, "concat", turn, 1)
+            for half in range(BANKS):
+                if half == 1 and live(turn - H_TURN):
+                    empty_bank(nc.scalar.copy, "g0", turn - H_TURN, 0)
+                    empty_bank(nc.scalar.copy, "g0", turn - H_TURN, 1)
+                if live(turn - FC1_TURN):
+                    silu(turn - FC1_TURN, 2 * half)
+                    silu(turn - FC1_TURN, 2 * half + 1)
             if live(turn - H_TURN):
-                empty_bank(nc.scalar.copy, "g0", turn - H_TURN, 0)
-                empty_bank(nc.scalar.copy, "g0", turn - H_TURN, 1)
                 regroup_h(turn - H_TURN)
             if live(turn):
                 quantise("concat", turn)
@@ -279,12 +287,8 @@ def tile_nnapprox_pa_t_kernel(
                 quantise("h", turn - H_TURN)
                 quantise("g0", turn - H_TURN)
 
-            for t in range(PACK):
-                if t == PACK // 2 and live(turn - FC2_TURN):
-                    fc2_minus(turn - FC2_TURN)
-                if live(turn - FC1_TURN):
-                    fc1(turn - FC1_TURN, t)
-                    silu(turn - FC1_TURN, t)
+            if live(turn - FC2_TURN):
+                fc2_minus(turn - FC2_TURN)
 
             if turn == CHUNKS + FC1_TURN:
                 finish(0, DONE_EARLY)

@@ -36,7 +36,7 @@ H_TURN = 2
 FC2_TURN = 3
 ABS_TURN = 4
 NORM_TURN = 5
-DONE_EARLY = (CHUNKS - 3) * CHUNK_TILES
+RUN = 8
 LOAD_AHEAD = 3
 
 
@@ -143,16 +143,16 @@ def tile_nnapprox_pa_t_kernel(
         def regroup_h(chunk):
             grouped = work.tile([P, CHUNK_TILES, P, PACK], BF16, name="h_grouped", tag="h_grouped", align_bytes=64)
             nc.vector.tensor_scalar(
-                out=grouped[:].rearrange("p r (c i) t -> p (r c) t i", i=4),
-                in0=tiles["h_t", chunk][:].rearrange("p t (c i) -> p c t i", i=4),
+                out=grouped[:].rearrange("p r (c i) t -> p (r c) t i", i=RUN),
+                in0=tiles["h_t", chunk][:].rearrange("p t (c i) -> p c t i", i=RUN),
                 scalar1=-1.0,
                 scalar2=None,
                 op0=ALU.mult,
             )
             tiles["h_grouped", chunk] = grouped
 
-        def fc2_minus(chunk):
-            bank = d_psum.tile([P, CHUNK], F32, name="d_bank", tag="d_bank")
+        def fc2_minus(chunk, pool, tag):
+            bank = pool.tile([P, CHUNK], F32, name=tag, tag=tag)
             pass_mx(bank, w2_words[:], weight_scales[:, HIDDEN : HIDDEN + OUT], "g0", chunk, True, False)
             pass_mx(bank, fc2_words[:], weight_scales[:, HIDDEN + OUT : HIDDEN + 2 * OUT], "h", chunk, False, True)
             tiles["d_bank", chunk] = bank
@@ -181,22 +181,6 @@ def tile_nnapprox_pa_t_kernel(
                     in_=tiles["m_bank", chunk][:, r, :],
                 )
 
-        def finish(first, last):
-            n = OUT // PARITIES
-            size = last - first
-            mean = stats[:, first:last, :, 1]
-            deviation = stats[:, first:last, :, 2]
-            squares = work.tile([P, size, PARITIES], F32, name="squares", tag="squares")
-            nc.vector.tensor_tensor(out=squares[:], in0=mean, in1=mean, op=ALU.mult)
-            means = work.tile([P, size], F32, name="means", tag="means")
-            nc.vector.tensor_tensor(out=means[:], in0=mean[:, :, 0], in1=mean[:, :, 1], op=ALU.add)
-            sums = work.tile([P, size, PARITIES], F32, name="sums", tag="sums")
-            nc.vector.scalar_tensor_tensor(out=sums[:], in0=squares[:], scalar=float(n), in1=deviation, op0=ALU.mult, op1=ALU.add)
-            nc.vector.tensor_scalar(out=l1[:, first:last], in0=means[:], scalar1=n / OUT, scalar2=None, op0=ALU.mult)
-            total = work.tile([P, size], F32, name="total", tag="total")
-            nc.vector.tensor_tensor(out=total[:], in0=sums[:, :, 0], in1=sums[:, :, 1], op=ALU.add)
-            nc.scalar.activation(out=l2[:, first:last], in_=total[:], func=ACT.Sqrt)
-
         def load_weight(words, scales, words_tile, first_col):
             cols = scales.shape[2]
             nc.sync.dma_start(out=words_tile[:].bitcast(I32), in_=words[0].bitcast(I32))
@@ -221,9 +205,9 @@ def tile_nnapprox_pa_t_kernel(
             nc.sync.dma_start(out=first_chunk[:, row_tiles, :], in_=concat_rows[:, row_tiles, :])
         tiles["concat", 0] = first_chunk
         load_weight(fc1_w_words, fc1_w_scales, fc1_words_in, 0)
+        load("concat", concat_rows, 1)
         fc1_bias = const.tile([P, PACK], BF16)
         nc.sync.dma_start(out=fc1_bias[:], in_=fc1_b.rearrange("(p t) -> p t", t=PACK))
-        load("concat", concat_rows, 1)
         load_weight(w2_0_words, w2_0_scales, w2_words, HIDDEN)
         load_weight(fc2_w_words, fc2_w_scales, fc2_words, HIDDEN + OUT)
         fc2_bias = const.tile([P, 1], BF16)
@@ -246,10 +230,8 @@ def tile_nnapprox_pa_t_kernel(
         )
 
         stats = const.tile([P, ROW_TILES, PARITIES, STATS], F32)
-        l2 = const.tile([P, ROW_TILES], F32)
-        l1 = const.tile([P, ROW_TILES], F32)
 
-        for turn in range(CHUNKS + NORM_TURN):
+        for turn in range(CHUNKS):
             if live(turn + LOAD_AHEAD):
                 load("concat", concat_rows, turn + LOAD_AHEAD)
             if live(turn - H_TURN + LOAD_AHEAD):
@@ -269,7 +251,7 @@ def tile_nnapprox_pa_t_kernel(
                 absolute(turn - ABS_TURN)
             if live(turn):
                 empty_bank(nc.vector.tensor_copy, "concat", turn, 0)
-                empty_bank(nc.vector.tensor_copy if turn % 2 == 0 else nc.scalar.copy, "concat", turn, 1)
+                empty_bank(nc.vector.tensor_copy if turn > 0 and turn % 2 == 0 else nc.scalar.copy, "concat", turn, 1)
             for half in range(BANKS):
                 if half == 1 and live(turn - H_TURN):
                     empty_bank(nc.scalar.copy, "g0", turn - H_TURN, 0)
@@ -288,11 +270,53 @@ def tile_nnapprox_pa_t_kernel(
                 quantise("g0", turn - H_TURN)
 
             if live(turn - FC2_TURN):
-                fc2_minus(turn - FC2_TURN)
+                fc2_minus(turn - FC2_TURN, d_psum, "d_bank")
 
-            if turn == CHUNKS + FC1_TURN:
-                finish(0, DONE_EARLY)
+        last = CHUNKS - 1
+        for t in range(PACK):
+            fc1(last, t)
+        for chunk in (last - 1, last):
+            transpose("g0", chunk)
+        absolute(last - 3)
+        for t in range(PACK):
+            silu(last, t)
+        for chunk in (last - 1, last):
+            empty_bank(nc.scalar.copy, "g0", chunk, 0)
+            empty_bank(nc.scalar.copy, "g0", chunk, 1)
+        regroup_h(last - 1)
+        quantise("h", last - 1)
+        fc2_minus(last - 2, d_psum, "d_bank")
+        transpose_back(last - 4)
+        transpose_back(last - 3)
+        regroup_h(last)
+        quantise("g0", last - 1)
+        quantise("h", last)
+        quantise("g0", last)
+        absolute(last - 2)
+        nc.scalar.activation(out=unread[:], in_=ident[:, 0:1], func=ACT.Sqrt)
+        fc2_minus(last - 1, h_psum, "h_bank")
+        transpose_back(last - 2)
+        absolute(last - 1)
+        fc2_minus(last, d_psum, "d_bank")
+        absolute(last)
+        transpose_back(last - 1)
+        transpose_back(last)
+        for chunk in range(last - 4, last + 1):
+            row_stats(chunk)
 
-        finish(DONE_EARLY, ROW_TILES)
+        n = OUT // PARITIES
+        mean = stats[:, :, :, 1]
+        squares = const.tile([P, ROW_TILES, PARITIES], F32)
+        nc.vector.tensor_tensor(out=squares[:], in0=mean, in1=mean, op=ALU.mult)
+        means = const.tile([P, ROW_TILES], F32)
+        nc.vector.tensor_tensor(out=means[:], in0=mean[:, :, 0], in1=mean[:, :, 1], op=ALU.add)
+        sums = const.tile([P, ROW_TILES, PARITIES], F32)
+        nc.vector.scalar_tensor_tensor(out=sums[:], in0=squares[:], scalar=float(n), in1=stats[:, :, :, 2], op0=ALU.mult, op1=ALU.add)
+        l1 = const.tile([P, ROW_TILES], F32)
+        nc.vector.tensor_scalar(out=l1[:], in0=means[:], scalar1=n / OUT, scalar2=None, op0=ALU.mult)
+        total = const.tile([P, ROW_TILES], F32)
+        nc.vector.tensor_tensor(out=total[:], in0=sums[:, :, 0], in1=sums[:, :, 1], op=ALU.add)
+        l2 = const.tile([P, ROW_TILES], F32)
+        nc.scalar.activation(out=l2[:], in_=total[:], func=ACT.Sqrt)
         nc.sync.dma_start(out=out_1.rearrange("(p r) -> p r", r=ROW_TILES), in_=l1[:])
         nc.sync.dma_start(out=out_0.rearrange("(p r) -> p r", r=ROW_TILES), in_=l2[:])

from contextlib import ExitStack

import concourse.mybir as mybir
from concourse.masks import make_identity

BF16 = mybir.dt.bfloat16
F32 = mybir.dt.float32
I32 = mybir.dt.int32
U32 = mybir.dt.uint32
U8 = mybir.dt.uint8
FP8X4 = mybir.dt.float8_e4m3fn_x4
FP4X4 = mybir.dt.float4_e2m1fn_x4
ACT = mybir.ActivationFunctionType
ALU = mybir.AluOpType

P = 128
PACK = 4
K = P * PACK
ROWS = 8192
HIDDEN = 512
OUT = 128
ROW_TILES = ROWS // P
CHUNK_TILES = 4
CHUNK = CHUNK_TILES * P
CHUNKS = ROW_TILES // CHUNK_TILES
WORDS = K // 2
BANK_TILES = 2
BANKS = CHUNK_TILES // BANK_TILES
PARITIES = 2
STATS = 3

FLOPS = 2 * ROWS * K * (OUT + HIDDEN + OUT)

FC1_TURN = 1
H_TURN = 2
FC2_TURN = 3
ABS_TURN = 4
NORM_TURN = 5
RUN = 8
LOAD_AHEAD = 3


def tile_nnapprox_pa_t_kernel(
    tc,
    g0,
    w2_0_words,
    w2_0_scales,
    wk_rest,
    fc1_w_words,
    fc1_w_scales,
    fc1_b,
    fc2_w_words,
    fc2_w_scales,
    fc2_b,
    out_0,
    out_1,
):
    nc = tc.nc
    g0_rows = g0.rearrange("(p r) k -> p r k", r=ROW_TILES)
    concat_rows = wk_rest.rearrange("(p r) n d -> p r (n d)", r=ROW_TILES)

    with ExitStack() as ctx:
        ctx.enter_context(tc.manual_schedule())
        const = ctx.enter_context(tc.tile_pool(name="const", bufs=1))
        loads = ctx.enter_context(tc.tile_pool(name="loads", bufs=LOAD_AHEAD + 1))
        work = ctx.enter_context(tc.tile_pool(name="work", bufs=3))
        t_psum = ctx.enter_context(tc.psum_pool(name="t_psum", bufs=3))
        h_psum = ctx.enter_context(tc.psum_pool(name="h_psum", bufs=PACK))
        d_psum = ctx.enter_context(tc.psum_pool(name="d_psum", bufs=1))

        tiles = {}

        def live(chunk):
            return 0 <= chunk < CHUNKS

        def load(name, rows, chunk):
            x = loads.tile([P, CHUNK_TILES, K], BF16, name=name, tag=name)
            first = chunk * CHUNK_TILES
            nc.sync.dma_start(out=x[:], in_=rows[:, first : first + CHUNK_TILES, :])
            tiles[name, chunk] = x

        def transpose(name, chunk):
            x = tiles[name, chunk]
            grouped = work.tile([P, CHUNK_TILES, P, PACK], BF16, name=name + "_grouped", tag=name + "_grouped", align_bytes=64)
            tiles[name + "_grouped", chunk] = grouped
            for half in range(BANKS):
                bank = t_psum.tile([P, BANK_TILES, 2, P], F32, name="t_bank", tag="t_bank")
                for r in range(BANK_TILES):
                    words = x[:, half * BANK_TILES + r, :].bitcast(F32)
                    for u in range(2):
                        nc.tensor.transpose(bank[:, r, u, :], words[:, u:WORDS:2], ident[:])
                tiles[name + "_bank", chunk, half] = bank

        def empty_bank(copy, name, chunk, half):
            bank = tiles[name + "_bank", chunk, half]
            grouped = tiles[name + "_grouped", chunk]
            first = half * BANK_TILES
            copy(
                out=grouped[:, first : first + BANK_TILES, :, :].bitcast(F32),
                in_=bank[:].rearrange("p r u b -> p r b u"),
            )

        def quantise(name, chunk):
            grouped = tiles[name + "_grouped", chunk]
            codes = work.tile([P, CHUNK], U32, name=name + "_codes", tag=name + "_codes", align_bytes=64)
            scales = work.tile([P, CHUNK], U8, name=name + "_scales", tag=name + "_scales", align_bytes=64)
            nc.vector.quantize_mx(
                out=codes[:].bitcast(FP8X4),
                scales=scales[:],
                in_=grouped[:].rearrange("p r b t -> p (r b t)"),
            )
            tiles[name + "_codes", chunk] = codes
            tiles[name + "_scales", chunk] = scales

        def pass_mx(bank, words, scales, name, chunk, start, stop):
            nc.tensor.matmul_mx(
                out=bank[:],
                lhsT=words.bitcast(FP4X4),
                lhsT_scale=scales,
                rhs=tiles[name + "_codes", chunk][:].bitcast(FP8X4),
                rhs_scale=tiles[name + "_scales", chunk][:],
                start=start,
                stop=stop,
            )

        def fc1(chunk, t):
            bank = h_psum.tile([P, CHUNK], F32, name="h_bank", tag="h_bank")
            words = fc1_words[:, 2 * P * t : 2 * P * (t + 1)]
            pass_mx(bank, words, fc1_scales[:, P * t : P * (t + 1)], "concat", chunk, True, True)
            tiles["h_bank", chunk, t] = bank

        def silu(chunk, t):
            if t == 0:
                tiles["h_t", chunk] = work.tile([P, PACK, CHUNK], BF16, name="h_t", tag="h_t")
            nc.scalar.activation(
                out=tiles["h_t", chunk][:, t, :],
                in_=tiles["h_bank", chunk, t][:],
                func=ACT.Silu,
                bias=fc1_bias[:, t : t + 1],
                scale=1.0,
            )

        def regroup_h(chunk):
            grouped = work.tile([P, CHUNK_TILES, P, PACK], BF16, name="h_grouped", tag="h_grouped", align_bytes=64)
            nc.vector.tensor_scalar(
                out=grouped[:].rearrange("p r (c i) t -> p (r c) t i", i=RUN),
                in0=tiles["h_t", chunk][:].rearrange("p t (c i) -> p c t i", i=RUN),
                scalar1=-1.0,
                scalar2=None,
                op0=ALU.mult,
            )
            tiles["h_grouped", chunk] = grouped

        def fc2_minus(chunk, pool, tag):
            bank = pool.tile([P, CHUNK], F32, name=tag, tag=tag)
            pass_mx(bank, w2_words[:], weight_scales[:, HIDDEN : HIDDEN + OUT], "g0", chunk, True, False)
            pass_mx(bank, fc2_words[:], weight_scales[:, HIDDEN + OUT : HIDDEN + 2 * OUT], "h", chunk, False, True)
            tiles["d_bank", chunk] = bank

        def absolute(chunk):
            magnitude = work.tile([P, CHUNK_TILES, P], F32, name="magnitude", tag="magnitude")
            nc.scalar.activation(
                out=magnitude[:].rearrange("p r b -> p (r b)"),
                in_=tiles["d_bank", chunk][:],
                func=ACT.Abs,
                bias=fc2_bias[:],
                scale=-1.0,
            )
            tiles["magnitude", chunk] = magnitude

        def transpose_back(chunk):
            bank = t_psum.tile([P, CHUNK_TILES, OUT], F32, name="t_bank", tag="t_bank")
            for r in range(CHUNK_TILES):
                nc.tensor.transpose(bank[:, r, :], tiles["magnitude", chunk][:, r, :], ident[:])
            tiles["m_bank", chunk] = bank

        def row_stats(chunk):
            for r in range(CHUNK_TILES):
                nc.vector.bn_stats(
                    out=stats[:, chunk * CHUNK_TILES + r, :, :].rearrange("p e s -> p (e s)"),
                    in_=tiles["m_bank", chunk][:, r, :],
                )

        def load_weight(words, scales, words_tile, first_col):
            cols = scales.shape[2]
            nc.sync.dma_start(out=words_tile[:].bitcast(I32), in_=words[0].bitcast(I32))
            for quad in range(4):
                nc.sync.dma_start(
                    out=weight_scales[32 * quad : 32 * quad + 4, first_col : first_col + cols].bitcast(I32),
                    in_=scales[0, 4 * quad : 4 * quad + 4, :].bitcast(I32),
                )

        ident = const.tile([P, P], F32)
        make_identity(nc, ident[:])

        weight_scales = const.tile([P, HIDDEN + 2 * OUT], U8, align_bytes=64)
        nc.vector.memset(weight_scales[:].bitcast(I32), 0)
        fc1_words_in = const.tile([P, 2 * HIDDEN], U8, align_bytes=64)
        w2_words = const.tile([P, 2 * OUT], U8, align_bytes=64)
        fc2_words = const.tile([P, 2 * OUT], U8, align_bytes=64)

        first_chunk = loads.tile([P, CHUNK_TILES, K], BF16, name="concat", tag="concat")
        for half in range(BANKS):
            row_tiles = slice(half * BANK_TILES, (half + 1) * BANK_TILES)
            nc.sync.dma_start(out=first_chunk[:, row_tiles, :], in_=concat_rows[:, row_tiles, :])
        tiles["concat", 0] = first_chunk
        load_weight(fc1_w_words, fc1_w_scales, fc1_words_in, 0)
        load("concat", concat_rows, 1)
        fc1_bias = const.tile([P, PACK], BF16)
        nc.sync.dma_start(out=fc1_bias[:], in_=fc1_b.rearrange("(p t) -> p t", t=PACK))
        load_weight(w2_0_words, w2_0_scales, w2_words, HIDDEN)
        load_weight(fc2_w_words, fc2_w_scales, fc2_words, HIDDEN + OUT)
        fc2_bias = const.tile([P, 1], BF16)
        nc.sync.dma_start(out=fc2_bias[:], in_=fc2_b.rearrange("(p o) -> p o", o=1))
        load("concat", concat_rows, 2)
        load("g0", g0_rows, 0)

        unread = const.tile([P, 1], F32)
        nc.scalar.activation(out=unread[:], in_=ident[:, 0:1], func=ACT.Silu)

        fc1_words = const.tile([P, 2 * HIDDEN], U8, align_bytes=64)
        nc.vector.tensor_copy(
            out=fc1_words[:].rearrange("p (t m e) -> p t m e", t=PACK, e=2),
            in_=fc1_words_in[:].rearrange("p (m t e) -> p t m e", t=PACK, e=2),
        )
        fc1_scales = const.tile([P, HIDDEN], U8, align_bytes=64)
        nc.vector.tensor_copy(
            out=fc1_scales[:].rearrange("p (t m) -> p t m", t=PACK),
            in_=weight_scales[:, 0:HIDDEN].rearrange("p (m t) -> p t m", t=PACK),
        )

        stats = const.tile([P, ROW_TILES, PARITIES, STATS], F32)

        for turn in range(CHUNKS):
            if live(turn + LOAD_AHEAD):
                load("concat", concat_rows, turn + LOAD_AHEAD)
            if live(turn - H_TURN + LOAD_AHEAD):
                load("g0", g0_rows, turn - H_TURN + LOAD_AHEAD)

            if live(turn):
                transpose("concat", turn)
            if live(turn - FC1_TURN):
                for t in range(PACK):
                    fc1(turn - FC1_TURN, t)
            if live(turn - H_TURN):
                transpose("g0", turn - H_TURN)
            if live(turn - NORM_TURN):
                transpose_back(turn - NORM_TURN)

            if live(turn - ABS_TURN):
                absolute(turn - ABS_TURN)
            if live(turn):
                empty_bank(nc.vector.tensor_copy, "concat", turn, 0)
                empty_bank(nc.vector.tensor_copy if turn > 0 and turn % 2 == 0 else nc.scalar.copy, "concat", turn, 1)
            for half in range(BANKS):
                if half == 1 and live(turn - H_TURN):
                    empty_bank(nc.scalar.copy, "g0", turn - H_TURN, 0)
                    empty_bank(nc.scalar.copy, "g0", turn - H_TURN, 1)
                if live(turn - FC1_TURN):
                    silu(turn - FC1_TURN, 2 * half)
                    silu(turn - FC1_TURN, 2 * half + 1)
            if live(turn - H_TURN):
                regroup_h(turn - H_TURN)
            if live(turn):
                quantise("concat", turn)
            if live(turn - NORM_TURN):
                row_stats(turn - NORM_TURN)
            if live(turn - H_TURN):
                quantise("h", turn - H_TURN)
                quantise("g0", turn - H_TURN)

            if live(turn - FC2_TURN):
                fc2_minus(turn - FC2_TURN, d_psum, "d_bank")

        last = CHUNKS - 1
        for t in range(PACK):
            fc1(last, t)
        for chunk in (last - 1, last):
            transpose("g0", chunk)
        absolute(last - 3)
        for t in range(PACK):
            silu(last, t)
        for chunk in (last - 1, last):
            empty_bank(nc.scalar.copy, "g0", chunk, 0)
            empty_bank(nc.scalar.copy, "g0", chunk, 1)
        regroup_h(last - 1)
        quantise("h", last - 1)
        fc2_minus(last - 2, d_psum, "d_bank")
        transpose_back(last - 4)
        transpose_back(last - 3)
        regroup_h(last)
        quantise("g0", last - 1)
        quantise("h", last)
        quantise("g0", last)
        absolute(last - 2)
        nc.scalar.activation(out=unread[:], in_=ident[:, 0:1], func=ACT.Sqrt)
        fc2_minus(last - 1, h_psum, "h_bank")
        transpose_back(last - 2)
        absolute(last - 1)
        fc2_minus(last, d_psum, "d_bank")
        absolute(last)
        transpose_back(last - 1)
        transpose_back(last)
        for chunk in range(last - 4, last + 1):
            row_stats(chunk)

        n = OUT // PARITIES
        mean = stats[:, :, :, 1]
        squares = const.tile([P, ROW_TILES, PARITIES], F32)
        nc.vector.tensor_tensor(out=squares[:], in0=mean, in1=mean, op=ALU.mult)
        means = const.tile([P, ROW_TILES], F32)
        nc.vector.tensor_tensor(out=means[:], in0=mean[:, :, 0], in1=mean[:, :, 1], op=ALU.add)
        sums = const.tile([P, ROW_TILES, PARITIES], F32)
        nc.vector.scalar_tensor_tensor(out=sums[:], in0=squares[:], scalar=float(n), in1=stats[:, :, :, 2], op0=ALU.mult, op1=ALU.add)
        l1 = const.tile([P, ROW_TILES], F32)
        nc.vector.tensor_scalar(out=l1[:], in0=means[:], scalar1=n / OUT, scalar2=None, op0=ALU.mult)
        total = const.tile([P, ROW_TILES], F32)
        nc.vector.tensor_tensor(out=total[:], in0=sums[:, :, 0], in1=sums[:, :, 1], op=ALU.add)
        l2 = const.tile([P, ROW_TILES], F32)
        nc.scalar.activation(out=l2[:], in_=total[:], func=ACT.Sqrt)
        nc.sync.dma_start(out=out_1.rearrange("(p r) -> p r", r=ROW_TILES), in_=l1[:])
        nc.sync.dma_start(out=out_0.rearrange("(p r) -> p r", r=ROW_TILES), in_=l2[:])
